import numpy as np
import ml_dtypes


def mxq(x, axis, fmt="e4m3"):
    dtype, down = {"e4m3": (ml_dtypes.float8_e4m3fn, 7), "e5m2": (ml_dtypes.float8_e5m2, 14)}[fmt]
    v = np.moveaxis(np.asarray(x, np.float32).astype(ml_dtypes.bfloat16).astype(np.float64), axis, -1)
    blocks = v.reshape(v.shape[:-1] + (-1, 32))
    amax = np.abs(blocks).max(-1, keepdims=True)
    byte = np.maximum(np.where(amax > 0, np.frexp(amax)[1] - 1 + 127, 0) - down, 1)
    scale = np.exp2(byte - 127.0)
    codes = (blocks / scale).astype(np.float32).astype(dtype).astype(np.float64)
    return np.moveaxis((codes * scale).reshape(v.shape), -1, axis)


WIDE = False


def mx_kscale(k):
    if not WIDE:
        return np.ones(k)
    levels = np.array([10, -10, 5, -5, 0])
    if k % 512:
        return np.exp2(np.random.permutation(np.resize(levels, k // 32))).repeat(32)
    a = np.empty((k // 512, 16))
    for p in range(k // 512):
        a[p, :8] = np.random.permutation(np.resize(levels, 8))
        for g in range(8):
            far = levels[np.abs(levels - a[p, g]) >= 10]
            a[p, g + 8] = far[np.random.randint(len(far))]
    return np.exp2(a.ravel()).repeat(32)


BF16 = ml_dtypes.bfloat16


def bf(x):
    return np.asarray(x, np.float32).astype(BF16)


def f64(x):
    return np.asarray(x).astype(np.float64)


B, N, C = 16, 16, 1024
BN_EPS = 1e-5


def bn(v):
    mean = v.mean(axis=(0, 2), keepdims=True)
    var = v.var(axis=(0, 2), keepdims=True)
    return (v - mean) / np.sqrt(var + BN_EPS)


def sigmoid(v):
    return 1.0 / (1.0 + np.exp(-v))


def softmax(v, axis):
    p = np.exp(v - v.max(axis=axis, keepdims=True))
    return p / p.sum(axis=axis, keepdims=True)


def draw_w(a, f):
    return bf(np.random.standard_normal((C, C)) * a / np.sqrt(C) / f[None, :])


def setup_inputs():
    s, t = mx_kscale(C), mx_kscale(C)
    s, t = s / s.max(), t / t.max()
    return {"x": bf(np.random.standard_normal((B, N, C)) * s),
            "edge": bf(np.random.standard_normal((B, N * N, C)) * t),
            "WA": draw_w(np.sqrt(2.0), s), "WB": draw_w(np.sqrt(2.0), s), "WE": draw_w(np.sqrt(2.0), t),
            "WU": draw_w(0.4, s), "WV": draw_w(0.5 * N, s)}


def reference(x, edge, WA, WB, WE, WU, WV):
    x, edge = f64(x), f64(edge)
    xq = mxq(x, 2, "e4m3")
    Vix = xq @ mxq(f64(WA), 1, "e4m3").T
    Vjx = xq @ mxq(f64(WB), 1, "e4m3").T
    e_proj = mxq(edge, 2, "e4m3") @ mxq(f64(WE), 1, "e4m3").T
    agg = np.repeat(Vix, N, axis=1) + np.tile(Vjx, (1, N, 1)) + e_proj
    edge_out = edge + np.maximum(bn(agg), 0.0)
    e = sigmoid(edge_out).reshape(B, N, N, C)
    e = softmax(e, 2).reshape(B, N * N, C)
    Ujx = np.tile(xq @ mxq(f64(WV), 1, "e4m3").T, (1, N, 1))
    Uix = xq @ mxq(f64(WU), 1, "e4m3").T
    msg = (e * Ujx).reshape(B, N, N, C).sum(axis=2)
    x_new = Uix + msg / N
    x_out = np.maximum(x + bn(x_new), 0.0)
    return x_out, edge_out

@@ -1,0 +1,575 @@
+from contextlib import ExitStack
+
+import concourse.mybir as mybir
+from concourse.masks import make_identity
+
+F32 = mybir.dt.float32
+BF16 = mybir.dt.bfloat16
+U32 = mybir.dt.uint32
+U8 = mybir.dt.uint8
+FP8X4 = mybir.dt.float8_e4m3fn_x4
+ALU = mybir.AluOpType
+ACTF = mybir.ActivationFunctionType
+AX = mybir.AxisListType
+
+P = 128
+C = 1024
+NJ = 16
+NT = 32
+HALF = 512
+EPS = 1e-5
+FLOPS = 2 * 1024 * 1024 * (4096 + 4 * 256)
+
+WU_FIRST_ROUND = 8
+
+
+def tile_graphmodel_pa_t_kernel(tc, x, edge, WA, WB, WE, WU, WV, out_0, out_1):
+    nc = tc.nc
+    with ExitStack() as ctx:
+        const = ctx.enter_context(tc.tile_pool(name="const", bufs=1))
+        stage = ctx.enter_context(tc.tile_pool(name="stage", bufs=2))
+        work = ctx.enter_context(tc.tile_pool(name="work", bufs=2))
+        small = ctx.enter_context(tc.tile_pool(name="small", bufs=3))
+        psum = ctx.enter_context(tc.psum_pool(name="psum", bufs=1))
+        ctx.enter_context(tc.manual_schedule())
+
+        xv = x.flatten_outer_dims().rearrange("(p h) c -> h p c", h=2)
+        o0 = out_0.flatten_outer_dims().rearrange("(p h) c -> h p c", h=2)
+        ev = edge.flatten_outer_dims().rearrange("(p h j) c -> h p j c", h=2, j=NJ)
+        o1 = out_1.flatten_outer_dims().rearrange("(p h j) c -> h p j c", h=2, j=NJ)
+        wdram = {"WA": WA, "WB": WB, "WE": WE, "WU": WU, "WV": WV}
+        wview = {}
+        for w in wdram:
+            wview[w] = wdram[w].rearrange("(a r p) k -> a p r k", a=4, r=2)
+
+        warm = const.tile([P, 1], F32, name="warm")
+        nc.vector.memset(warm[:], 0.0)
+        warm2 = const.tile([P, 1], F32, name="warm2")
+        nc.scalar.activation(out=warm2[:], in_=warm[:], func=ACTF.Exp)
+        mhalf = const.tile([P, 1], F32, name="mhalf")
+        nc.vector.memset(mhalf[:], -0.5)
+        epst = const.tile([P, 1], F32, name="epst")
+        nc.vector.memset(epst[:], EPS)
+        ident = const.tile([P, P], F32, name="ident")
+        make_identity(nc, ident[:])
+        rsel = const.tile([P, 8], F32, name="rsel")
+        nc.vector.tensor_reduce(
+            out=rsel[:], in_=ident[:].rearrange("p (a r) -> p r a", r=8), axis=AX.X, op=ALU.add
+        )
+        negg = const.tile([P, P], F32, name="negg")
+        nc.vector.tensor_scalar(
+            out=negg[:].rearrange("p (a r) -> p a r", r=8),
+            in0=rsel[:].unsqueeze(1).to_broadcast([P, 16, 8]),
+            scalar1=-1.0 / 16.0,
+            scalar2=None,
+            op0=ALU.mult,
+        )
+
+        wc = {}
+        ws = {}
+        for w in wdram:
+            wc[w] = const.tile([P, 2, C], U32, name="wc" + w, align_bytes=64)
+            ws[w] = const.tile([P, 2, C], U8, name="ws" + w, align_bytes=64)
+        xn = const.tile([P, 2, C], BF16, name="xn")
+        gx = const.tile([P, 2, 2, 512], BF16, name="gx", align_bytes=64)
+        xc = const.tile([P, 2, 2, P], U32, name="xc", align_bytes=64)
+        xs = const.tile([P, 2, 2, P], U8, name="xs", align_bytes=64)
+        xrc = const.tile([P, NJ, 2, P], U32, name="xrc", align_bytes=64)
+        xrs = const.tile([P, NJ, 2, P], U8, name="xrs", align_bytes=64)
+        den = [const.tile([P, C], F32, name="den%d" % h) for h in range(2)]
+        num = [const.tile([P, C], F32, name="num%d" % h) for h in range(2)]
+
+        def transposes(src_f32, tag, bufs):
+            bank = psum.tile([P, HALF], F32, name="bank_" + tag, tag=tag, bufs=bufs)
+            for g in range(2):
+                for u in range(2):
+                    cols = slice((2 * g + u) * P, (2 * g + u + 1) * P)
+                    words = src_f32[:, 256 * g + u : 256 * (g + 1) : 2]
+                    nc.tensor.transpose(bank[:, cols], words, ident[:])
+            return bank
+
+        def regroup(dst_f32, bank):
+            nc.scalar.copy(out=dst_f32, in_=bank[:].rearrange("q (g u r) -> q g r u", g=2, u=2))
+
+        def mx(out, lc, ls, rc, rs, start, stop):
+            nc.tensor.matmul_mx(
+                out=out,
+                lhsT=lc.bitcast(FP8X4),
+                lhsT_scale=ls,
+                rhs=rc.bitcast(FP8X4),
+                rhs_scale=rs,
+                start=start,
+                stop=stop,
+            )
+
+        wn = {}
+
+        def load_w(w, a):
+            t = stage.tile([P, 2, C], BF16, name="wn", tag="wn", bufs=4)
+            nc.sync.dma_start(out=t[:], in_=wview[w][a])
+            wn[(w, a)] = t
+
+        ech = {}
+
+        def load_e1(jc, h):
+            t = stage.tile([P, 2, C], BF16, name="ech", tag="ech", bufs=6)
+            nc.sync.dma_start(out=t[:], in_=ev[h][:, 2 * jc : 2 * jc + 2, :])
+            ech[(h, jc)] = t
+
+        def load_e(jc):
+            for h in range(2):
+                load_e1(jc, h)
+
+        for h in range(2):
+            nc.sync.dma_start(out=xn[:, h, :], in_=xv[h])
+        load_e1(0, 0)
+
+        gwt = {}
+        ubank = {}
+
+        def unit_t(w, a, r2, tag, bufs):
+            ubank[(w, a, r2)] = transposes(wn[(w, a)][:].bitcast(F32)[:, r2, :], tag, bufs)
+
+        def unit_r(w, a, r2):
+            gwf = gwt[(w, a // 2)][:].bitcast(F32).rearrange("q g (r u) -> q g r u", u=2)
+            r0 = ((a % 2) * 2 + r2) * P
+            regroup(gwf[:, :, r0 : r0 + P, :], ubank[(w, a, r2)])
+
+        def new_gw(w, n2):
+            gwt[(w, n2)] = stage.tile([P, 2, 2048], BF16, name="gw", tag="gw", bufs=3, align_bytes=64)
+
+        def prep_w(w, a, tags):
+            if a % 2 == 0:
+                new_gw(w, a // 2)
+            for r2 in range(2):
+                tag, bufs = tags[r2 % len(tags)]
+                unit_t(w, a, r2, tag, bufs)
+                unit_r(w, a, r2)
+
+        def quant_w(w, n2):
+            cols = slice(n2 * HALF, (n2 + 1) * HALF)
+            for g in range(2):
+                nc.vector.quantize_mx(
+                    out=wc[w][:, g, cols].bitcast(FP8X4),
+                    scales=ws[w][:, g, cols],
+                    in_=gwt[(w, n2)][:, g, :],
+                )
+
+        grxt = {}
+
+        def xrep_copy(a, jj, on_scalar):
+            if jj == 0:
+                grxt[a] = stage.tile([P, 4, 2, 512], BF16, name="grx", tag="gw", bufs=3, align_bytes=64)
+            grf = grxt[a][:].bitcast(F32)
+            gxf = gx[:].bitcast(F32)
+            j = 4 * a + jj
+            for g in range(2):
+                src = gxf[:, j % 2, g, :].rearrange("q (b l u) -> q b l u", b=16, l=8)[:, :, j // 2, :]
+                dst = grf[:, jj, g, :].rearrange("q (b i u) -> q b i u", b=16, i=8)
+                if on_scalar:
+                    nc.scalar.copy(out=dst, in_=src.unsqueeze(2).to_broadcast([P, 16, 8, 2]))
+                else:
+                    nc.vector.tensor_copy(out=dst, in_=src.unsqueeze(2).to_broadcast([P, 16, 8, 2]))
+
+        def xrep_quant(a):
+            nc.vector.quantize_mx(
+                out=xrc[:, 4 * a : 4 * a + 4, :, :].rearrange("q j g r -> q (j g r)").bitcast(FP8X4),
+                scales=xrs[:, 4 * a : 4 * a + 4, :, :].rearrange("q j g r -> q (j g r)"),
+                in_=grxt[a][:].rearrange("q j g w -> q (j g w)"),
+            )
+
+        bstt = {}
+        mvt = {}
+        pst = {}
+        nmt = {}
+        rstd = {}
+        nbt = {}
+
+        def stats_bn(key, n2, src):
+            if n2 == 0:
+                bstt[key] = small.tile([P, 12], F32, name="bst", tag="bst", bufs=3)
+            nc.vector.bn_stats(out=bstt[key][:, 6 * n2 : 6 * n2 + 6], in_=src)
+
+        def stats_aggr(key):
+            mvt[key] = small.tile([P, 3], F32, name="mv", tag="mv", bufs=3)
+            nc.vector.bn_aggr(out=mvt[key][:, 0:2], in_=bstt[key][:])
+
+        def stats_e2(key):
+            mv = mvt[key]
+            nc.vector.tensor_scalar(
+                out=mv[:, 2:3], in0=mv[:, 0:1], scalar1=mv[:, 0:1], scalar2=mv[:, 1:2], op0=ALU.mult, op1=ALU.add
+            )
+
+        def stats_sum(key):
+            pst[key] = psum.tile([P, HALF], F32, name="st", tag="st", bufs=1)
+            nc.tensor.matmul(out=pst[key][:, 0:3], lhsT=negg[:], rhs=mvt[key][:], start=True, stop=True)
+
+        def stats_out(key):
+            nmt[key] = small.tile([P, 3], F32, name="nm", tag="nm", bufs=4)
+            nc.scalar.copy(out=nmt[key][:], in_=pst[key][:, 0:3])
+
+        def stats_rstd(key, want_nb=False):
+            nm = nmt[key]
+            t1 = small.tile([P, 1], F32, name="t1", tag="t1", bufs=3)
+            nc.scalar.activation(out=t1[:], in_=nm[:, 0:1], func=ACTF.Identity, scale=nm[:, 0:1], bias=nm[:, 2:3])
+            u1 = small.tile([P, 1], F32, name="u1", tag="u1", bufs=3)
+            nc.scalar.activation(out=u1[:], in_=t1[:], func=ACTF.Identity, scale=-1.0, bias=epst[:, 0:1])
+            rstd[key] = small.tile([P, 1], F32, name="rstd", tag="rstd", bufs=4)
+            nc.gpsimd.tensor_tensor(out=rstd[key][:], in0=u1[:], in1=mhalf[:], op=ALU.pow)
+            if want_nb:
+                nbt[key] = small.tile([P, 1], F32, name="nb", tag="nb", bufs=2)
+                nc.gpsimd.tensor_tensor(out=nbt[key][:], in0=nm[:, 0:1], in1=rstd[key][:], op=ALU.mult)
+
+        trb = {}
+        ge = {}
+        ecs = {}
+        acc = {}
+        rz = {}
+        tet = {}
+        et = {}
+        mt = {}
+        ubt = {}
+
+        def ok(t):
+            return 0 <= t < NT
+
+        def t_transpose(t, tag="tr", bufs=1):
+            if not ok(t):
+                return
+            j, h = t // 2, t % 2
+            ef = ech[(h, j // 2)][:].bitcast(F32)
+            trb[t] = transposes(ef[:, j % 2, :], tag, bufs)
+
+        def t_regroup(t):
+            if not ok(t):
+                return
+            ge[t] = stage.tile([P, 2, 512], BF16, name="ge", tag="ge", bufs=3, align_bytes=64)
+            regroup(ge[t][:].bitcast(F32).rearrange("q g (r u) -> q g r u", u=2), trb[t])
+
+        def t_quantise(t):
+            if not ok(t):
+                return
+            c_ = stage.tile([P, 2, P], U32, name="ec", tag="ec", bufs=4, align_bytes=64)
+            s_ = stage.tile([P, 2, P], U8, name="es", tag="es", bufs=4, align_bytes=64)
+            nc.vector.quantize_mx(
+                out=c_[:].rearrange("q g r -> q (g r)").bitcast(FP8X4),
+                scales=s_[:].rearrange("q g r -> q (g r)"),
+                in_=ge[t][:].rearrange("q g w -> q (g w)"),
+            )
+            ecs[t] = (c_, s_)
+
+        def t_agg(t, n2):
+            if not ok(t):
+                return
+            j, h = t // 2, t % 2
+            a_ = psum.tile([P, HALF], F32, name="acc", tag="acc", bufs=4)
+            acc[(t, n2)] = a_
+            cols = slice(n2 * HALF, (n2 + 1) * HALF)
+            c_, s_ = ecs[t]
+            ops = [
+                (c_, s_, "WE"),
+                (xc[:, h], xs[:, h], "WA"),
+                (xrc[:, j], xrs[:, j], "WB"),
+            ]
+            i = 0
+            for lc, ls, w in ops:
+                for g in range(2):
+                    mx(a_[:], lc[:, g, :], ls[:, g, :], wc[w][:, g, cols], ws[w][:, g, cols], i == 0, i == 5)
+                    i += 1
+
+        def t_bn(t, n2):
+            if ok(t):
+                stats_bn(t, n2, acc[(t, n2)][:])
+
+        def t_aggr(t):
+            if ok(t):
+                stats_aggr(t)
+
+        def t_e2(t):
+            if ok(t):
+                stats_e2(t)
+
+        def t_sum(t):
+            if ok(t):
+                stats_sum(t)
+
+        def t_out(t):
+            if ok(t):
+                stats_out(t)
+
+        def t_rstd(t):
+            if ok(t):
+                stats_rstd(t)
+
+        def t_relu(t, n2):
+            if not ok(t):
+                return
+            if n2 == 0:
+                rz[t] = work.tile([P, C], F32, name="rz", tag="rz", bufs=5)
+            cols = slice(n2 * HALF, (n2 + 1) * HALF)
+            nc.scalar.activation(
+                out=rz[t][:, cols], in_=acc[(t, n2)][:], func=ACTF.Relu, bias=nmt[t][:, 0:1], scale=1.0
+            )
+
+        def t_edge_out(t):
+            if not ok(t):
+                return
+            j, h = t // 2, t % 2
+            nc.vector.scalar_tensor_tensor(
+                out=rz[t][:],
+                in0=rz[t][:],
+                scalar=rstd[t][:, 0:1],
+                in1=ech[(h, j // 2)][:, j % 2, :],
+                op0=ALU.mult,
+                op1=ALU.add,
+            )
+            nc.sync.dma_start(out=o1[h][:, j, :], in_=rz[t][:])
+
+        def t_tanh(t):
+            if not ok(t):
+                return
+            tet[t] = work.tile([P, C], F32, name="te", tag="te", bufs=3)
+            nc.scalar.activation(out=tet[t][:], in_=rz[t][:], func=ACTF.Tanh, scale=0.5)
+
+        def t_exp(t):
+            if not ok(t):
+                return
+            j, h = t // 2, t % 2
+            et[t] = den[h] if j == 0 else tet[t]
+            nc.scalar.activation(out=et[t][:], in_=tet[t][:], func=ACTF.Exp, scale=0.5)
+            if t == NT - 1:
+                nc.scalar.activation(out=warm2[:], in_=epst[:], func=ACTF.Ln)
+
+        def u_node(j):
+            if not 0 <= j < NJ:
+                return
+            for n2 in range(2):
+                u_ = psum.tile([P, HALF], F32, name="ub", tag="ub", bufs=2)
+                cols = slice(n2 * HALF, (n2 + 1) * HALF)
+                for g in range(2):
+                    mx(u_[:], xrc[:, j, g, :], xrs[:, j, g, :], wc["WV"][:, g, cols], ws["WV"][:, g, cols], g == 0, g == 1)
+                ubt[(j, n2)] = u_
+
+        def t_prod(t, n2):
+            if not ok(t):
+                return
+            j, h = t // 2, t % 2
+            if n2 == 0:
+                mt[t] = num[h] if j == 0 else work.tile([P, C], F32, name="mt", tag="mt", bufs=2)
+            cols = slice(n2 * HALF, (n2 + 1) * HALF)
+            nc.vector.tensor_tensor(out=mt[t][:, cols], in0=et[t][:, cols], in1=ubt[(j, n2)][:], op=ALU.mult)
+
+        def t_den(t):
+            if not ok(t) or t < 2:
+                return
+            h = t % 2
+            eng = nc.vector if t >= NT - 4 else nc.gpsimd
+            eng.tensor_tensor(out=den[h][:], in0=den[h][:], in1=et[t][:], op=ALU.add)
+
+        def t_num(t):
+            if not ok(t) or t < 2:
+                return
+            h = t % 2
+            nc.vector.tensor_tensor(out=num[h][:], in0=num[h][:], in1=mt[t][:], op=ALU.add)
+
+        start_tags = [("acc", 4), ("ub", 2)]
+        for n2 in range(2):
+            for w in ("WE", "WA", "WB"):
+                load_w(w, 2 * n2)
+                load_w(w, 2 * n2 + 1)
+                if n2 == 0 and w == "WE":
+                    gxf0 = gx[:].bitcast(F32)
+                    xf = xn[:].bitcast(F32)
+                    for h in range(2):
+                        bank = transposes(xf[:, h, :], "acc", 4)
+                        regroup(gxf0[:, h, :, :].rearrange("q g (r u) -> q g r u", u=2), bank)
+                    nc.vector.quantize_mx(
+                        out=xc[:].rearrange("q h g r -> q (h g r)").bitcast(FP8X4),
+                        scales=xs[:].rearrange("q h g r -> q (h g r)"),
+                        in_=gx[:].rearrange("q h g w -> q (h g w)"),
+                    )
+                    t_transpose(0, "acc", 4)
+                    t_regroup(0)
+                    for jj in range(4):
+                        xrep_copy(0, jj, False)
+                    t_quantise(0)
+                    xrep_quant(0)
+                    t_transpose(2)
+                prep_w(w, 2 * n2, start_tags)
+                prep_w(w, 2 * n2 + 1, start_tags)
+                quant_w(w, n2)
+        load_e1(0, 1)
+        load_e(1)
+        for a in range(4):
+            load_w("WV", a)
+        load_e(2)
+
+        uix = {}
+
+        def x_wu():
+            for h in range(2):
+                for n2 in range(2):
+                    u_ = psum.tile([P, HALF], F32, name="uix", tag="acc", bufs=4)
+                    cols = slice(n2 * HALF, (n2 + 1) * HALF)
+                    for g in range(2):
+                        mx(u_[:], xc[:, h, g, :], xs[:, h, g, :], wc["WU"][:, g, cols], ws["WU"][:, g, cols], g == 0, g == 1)
+                    uix[(h, n2)] = u_
+
+        def wu_unit(k):
+            u = (k - WU_FIRST_ROUND) // 2
+            if (k - WU_FIRST_ROUND) % 2 != 0 or not 0 <= u < 8:
+                return None
+            return (u // 2, u % 2)
+
+        for k in range(NT):
+            t_exp(k - 4)
+            t_regroup(k + 2)
+            t_agg(k, 0)
+            t_bn(k, 0)
+            t_sum(k - 1)
+            t_prod(k - 4, 0)
+            t_den(k - 4)
+            t_out(k - 1)
+            t_relu(k - 1, 0)
+            t_agg(k, 1)
+            t_prod(k - 4, 1)
+            t_rstd(k - 1)
+            t_relu(k - 1, 1)
+            t_bn(k, 1)
+            t_aggr(k)
+            t_edge_out(k - 2)
+            t_e2(k)
+            if k in (1, 2):
+                quant_w("WV", k - 1)
+            if k in (WU_FIRST_ROUND + 8, WU_FIRST_ROUND + 16):
+                quant_w("WU", (k - WU_FIRST_ROUND) // 8 - 1)
+            t_transpose(k + 3)
+            if k % 2 == 1:
+                u_node((k - 3) // 2)
+            un = wu_unit(k)
+            if un is not None:
+                if un[0] % 2 == 0 and un[1] == 0:
+                    new_gw("WU", un[0] // 2)
+                unit_t("WU", un[0], un[1], "st", 1)
+            t_quantise(k + 2)
+            t_tanh(k - 3)
+            t_num(k - 4)
+            if un is not None:
+                unit_r("WU", un[0], un[1])
+            for a in (1, 2, 3):
+                if 8 * a - 7 <= k <= 8 * a - 4:
+                    xrep_copy(a, k - (8 * a - 7), True)
+                if k == 8 * a - 3:
+                    xrep_quant(a)
+            if k == 0:
+                t_transpose(1, "ub", 2)
+                t_regroup(1)
+                t_quantise(1)
+            if k < 2:
+                for u in range(4 * k, 4 * k + 4):
+                    if u % 4 == 0:
+                        new_gw("WV", u // 4)
+                    unit_t("WV", u // 2, u % 2, "ub", 2)
+                    unit_r("WV", u // 2, u % 2)
+            if k == 3:
+                for a in range(4):
+                    load_w("WU", a)
+            if k % 4 == 1 and 3 <= (k + 7) // 4 < NJ // 2:
+                load_e((k + 7) // 4)
+
+        t_exp(NT - 4)
+        t_sum(NT - 1)
+        t_edge_out(NT - 2)
+        t_tanh(NT - 3)
+        t_out(NT - 1)
+        t_relu(NT - 1, 0)
+        t_relu(NT - 1, 1)
+        t_rstd(NT - 1)
+        t_den(NT - 4)
+        t_prod(NT - 4, 0)
+        t_prod(NT - 4, 1)
+        t_exp(NT - 3)
+        t_num(NT - 4)
+        t_tanh(NT - 2)
+        t_edge_out(NT - 1)
+        t_den(NT - 3)
+        t_exp(NT - 2)
+        t_tanh(NT - 1)
+        t_den(NT - 2)
+        t_prod(NT - 3, 0)
+        t_prod(NT - 3, 1)
+        u_node(NJ - 1)
+        x_wu()
+        t_exp(NT - 1)
+        t_den(NT - 1)
+        t_num(NT - 3)
+        for t in (NT - 2, NT - 1):
+            t_prod(t, 0)
+            t_prod(t, 1)
+            t_num(t)
+
+        units = [(h, n2) for h in range(2) for n2 in range(2)]
+        xnew = {}
+        for h in range(2):
+            xnew[h] = work.tile([P, C], F32, name="xnew", tag="rz", bufs=5)
+        for h, n2 in units:
+            cols = slice(n2 * HALF, (n2 + 1) * HALF)
+            nc.scalar.activation(out=den[h][:, cols], in_=den[h][:, cols], func=ACTF.Ln)
+        for h, n2 in units:
+            cols = slice(n2 * HALF, (n2 + 1) * HALF)
+            nc.scalar.activation(out=den[h][:, cols], in_=den[h][:, cols], func=ACTF.Exp, scale=-1.0)
+
+        def tail_mul(h, n2):
+            cols = slice(n2 * HALF, (n2 + 1) * HALF)
+            eng = nc.gpsimd if h == 1 else nc.vector
+            eng.tensor_tensor(out=num[h][:, cols], in0=num[h][:, cols], in1=den[h][:, cols], op=ALU.mult)
+
+        def tail_add(h, n2):
+            cols = slice(n2 * HALF, (n2 + 1) * HALF)
+            nc.vector.scalar_tensor_tensor(
+                out=xnew[h][:, cols],
+                in0=num[h][:, cols],
+                scalar=1.0 / 16.0,
+                in1=uix[(h, n2)][:],
+                op0=ALU.mult,
+                op1=ALU.add,
+            )
+
+        def tail_bn(h, n2):
+            cols = slice(n2 * HALF, (n2 + 1) * HALF)
+            stats_bn(("x", h), n2, xnew[h][:, cols])
+
+        for f in (tail_mul, tail_add, tail_bn):
+            f(0, 0)
+            f(0, 1)
+        tail_mul(1, 0)
+        stats_aggr(("x", 0))
+        tail_mul(1, 1)
+        stats_e2(("x", 0))
+        stats_sum(("x", 0))
+        stats_out(("x", 0))
+        stats_rstd(("x", 0), True)
+        for f in (tail_add, tail_bn):
+            f(1, 0)
+            f(1, 1)
+        stats_aggr(("x", 1))
+        stats_e2(("x", 1))
+        stats_sum(("x", 1))
+        stats_out(("x", 1))
+        stats_rstd(("x", 1), True)
+        for h in range(2):
+            key = ("x", h)
+            for n2 in range(2):
+                cols = slice(n2 * HALF, (n2 + 1) * HALF)
+                nc.vector.scalar_tensor_tensor(
+                    out=xnew[h][:, cols],
+                    in0=xnew[h][:, cols],
+                    scalar=rstd[key][:, 0:1],
+                    in1=xn[:, h, cols],
+                    op0=ALU.mult,
+                    op1=ALU.add,
+                )
+                nc.scalar.activation(
+                    out=xnew[h][:, cols], in_=xnew[h][:, cols], func=ACTF.Relu, bias=nbt[key][:, 0:1], scale=1.0
+                )
+                nc.sync.dma_start(out=o0[h][:, cols], in_=xnew[h][:, cols])

@@ -18,9 +18,14 @@ NJ = 16
 NT = 32
 HALF = 512
 EPS = 1e-5
+SPLIT = 2
 FLOPS = 2 * 1024 * 1024 * (4096 + 4 * 256)
 
-WU_FIRST_ROUND = 8
+TAIL_NODES = 2
+XREP = (((2, 0), (2, 1), (2, 2)), ((2, 3), (3, 0), (3, 1)), ((3, 2), (3, 3)))
+DEN_POOL = 768
+WV_UNITS = ((0, 1, 2), (3, 4, 5), (6, 7))
+WU_FIRST_ROUND = 9
 
 
 def tile_graphmodel_pa_t_kernel(tc, x, edge, WA, WB, WE, WU, WV, out_0, out_1):
@@ -88,8 +93,12 @@ def tile_graphmodel_pa_t_kernel(tc, x, edge, WA, WB, WE, WU, WV, out_0, out_1):
                     nc.tensor.transpose(bank[:, cols], words, ident[:])
             return bank
 
-        def regroup(dst_f32, bank):
-            nc.scalar.copy(out=dst_f32, in_=bank[:].rearrange("q (g u r) -> q g r u", g=2, u=2))
+        def regroup(dst_f32, bank, on_vector=False):
+            src = bank[:].rearrange("q (g u r) -> q g r u", g=2, u=2)
+            if on_vector:
+                nc.vector.tensor_copy(out=dst_f32, in_=src)
+            else:
+                nc.scalar.copy(out=dst_f32, in_=src)
 
         def mx(out, lc, ls, rc, rs, start, stop):
             nc.tensor.matmul_mx(
@@ -111,18 +120,15 @@ def tile_graphmodel_pa_t_kernel(tc, x, edge, WA, WB, WE, WU, WV, out_0, out_1):
 
         ech = {}
 
-        def load_e1(jc, h):
-            t = stage.tile([P, 2, C], BF16, name="ech", tag="ech", bufs=6)
-            nc.sync.dma_start(out=t[:], in_=ev[h][:, 2 * jc : 2 * jc + 2, :])
-            ech[(h, jc)] = t
-
-        def load_e(jc):
+        def load_e(jc, j0=0, j1=2):
             for h in range(2):
-                load_e1(jc, h)
+                if j0 == 0:
+                    ech[(h, jc)] = stage.tile([P, 2, C], BF16, name="ech", tag="ech", bufs=6)
+                nc.sync.dma_start(out=ech[(h, jc)][:, j0:j1, :], in_=ev[h][:, 2 * jc + j0 : 2 * jc + j1, :])
 
         for h in range(2):
             nc.sync.dma_start(out=xn[:, h, :], in_=xv[h])
-        load_e1(0, 0)
+        load_e(0, 0, 1)
 
         gwt = {}
         ubank = {}
@@ -130,10 +136,10 @@ def tile_graphmodel_pa_t_kernel(tc, x, edge, WA, WB, WE, WU, WV, out_0, out_1):
         def unit_t(w, a, r2, tag, bufs):
             ubank[(w, a, r2)] = transposes(wn[(w, a)][:].bitcast(F32)[:, r2, :], tag, bufs)
 
-        def unit_r(w, a, r2):
+        def unit_r(w, a, r2, on_vector=False):
             gwf = gwt[(w, a // 2)][:].bitcast(F32).rearrange("q g (r u) -> q g r u", u=2)
             r0 = ((a % 2) * 2 + r2) * P
-            regroup(gwf[:, :, r0 : r0 + P, :], ubank[(w, a, r2)])
+            regroup(gwf[:, :, r0 : r0 + P, :], ubank[(w, a, r2)], on_vector)
 
         def new_gw(w, n2):
             gwt[(w, n2)] = stage.tile([P, 2, 2048], BF16, name="gw", tag="gw", bufs=3, align_bytes=64)
@@ -144,7 +150,7 @@ def tile_graphmodel_pa_t_kernel(tc, x, edge, WA, WB, WE, WU, WV, out_0, out_1):
             for r2 in range(2):
                 tag, bufs = tags[r2 % len(tags)]
                 unit_t(w, a, r2, tag, bufs)
-                unit_r(w, a, r2)
+                unit_r(w, a, r2, w == "WB" and a == 3 and r2 == 1)
 
         def quant_w(w, n2):
             cols = slice(n2 * HALF, (n2 + 1) * HALF)
@@ -157,19 +163,18 @@ def tile_graphmodel_pa_t_kernel(tc, x, edge, WA, WB, WE, WU, WV, out_0, out_1):
 
         grxt = {}
 
-        def xrep_copy(a, jj, on_scalar):
-            if jj == 0:
+        def xrep_copy(a, jj, g, on_scalar):
+            if jj == 0 and g == 0:
                 grxt[a] = stage.tile([P, 4, 2, 512], BF16, name="grx", tag="gw", bufs=3, align_bytes=64)
             grf = grxt[a][:].bitcast(F32)
             gxf = gx[:].bitcast(F32)
             j = 4 * a + jj
-            for g in range(2):
-                src = gxf[:, j % 2, g, :].rearrange("q (b l u) -> q b l u", b=16, l=8)[:, :, j // 2, :]
-                dst = grf[:, jj, g, :].rearrange("q (b i u) -> q b i u", b=16, i=8)
-                if on_scalar:
-                    nc.scalar.copy(out=dst, in_=src.unsqueeze(2).to_broadcast([P, 16, 8, 2]))
-                else:
-                    nc.vector.tensor_copy(out=dst, in_=src.unsqueeze(2).to_broadcast([P, 16, 8, 2]))
+            src = gxf[:, j % 2, g, :].rearrange("q (b l u) -> q b l u", b=16, l=8)[:, :, j // 2, :]
+            dst = grf[:, jj, g, :].rearrange("q (b i u) -> q b i u", b=16, i=8)
+            if on_scalar:
+                nc.scalar.copy(out=dst, in_=src.unsqueeze(2).to_broadcast([P, 16, 8, 2]))
+            else:
+                nc.vector.tensor_copy(out=dst, in_=src.unsqueeze(2).to_broadcast([P, 16, 8, 2]))
 
         def xrep_quant(a):
             nc.vector.quantize_mx(
@@ -182,6 +187,7 @@ def tile_graphmodel_pa_t_kernel(tc, x, edge, WA, WB, WE, WU, WV, out_0, out_1):
         mvt = {}
         pst = {}
         nmt = {}
+        negvar = {}
         rstd = {}
         nbt = {}
 
@@ -196,8 +202,8 @@ def tile_graphmodel_pa_t_kernel(tc, x, edge, WA, WB, WE, WU, WV, out_0, out_1):
 
         def stats_e2(key):
             mv = mvt[key]
-            nc.vector.tensor_scalar(
-                out=mv[:, 2:3], in0=mv[:, 0:1], scalar1=mv[:, 0:1], scalar2=mv[:, 1:2], op0=ALU.mult, op1=ALU.add
+            nc.scalar.activation(
+                out=mv[:, 2:3], in_=mv[:, 0:1], func=ACTF.Identity, scale=mv[:, 0:1], bias=mv[:, 1:2]
             )
 
         def stats_sum(key):
@@ -208,18 +214,27 @@ def tile_graphmodel_pa_t_kernel(tc, x, edge, WA, WB, WE, WU, WV, out_0, out_1):
             nmt[key] = small.tile([P, 3], F32, name="nm", tag="nm", bufs=4)
             nc.scalar.copy(out=nmt[key][:], in_=pst[key][:, 0:3])
 
+        def stats_negvar(key):
+            nm = nmt[key]
+            negvar[key] = small.tile([P, 1], F32, name="negvar", tag="negvar", bufs=3)
+            nc.scalar.activation(
+                out=negvar[key][:], in_=nm[:, 0:1], func=ACTF.Identity, scale=nm[:, 0:1], bias=nm[:, 2:3]
+            )
+
         def stats_rstd(key, want_nb=False):
             nm = nmt[key]
-            t1 = small.tile([P, 1], F32, name="t1", tag="t1", bufs=3)
-            nc.scalar.activation(out=t1[:], in_=nm[:, 0:1], func=ACTF.Identity, scale=nm[:, 0:1], bias=nm[:, 2:3])
-            u1 = small.tile([P, 1], F32, name="u1", tag="u1", bufs=3)
-            nc.scalar.activation(out=u1[:], in_=t1[:], func=ACTF.Identity, scale=-1.0, bias=epst[:, 0:1])
+            vareps = small.tile([P, 1], F32, name="vareps", tag="vareps", bufs=3)
+            nc.scalar.activation(
+                out=vareps[:], in_=negvar[key][:], func=ACTF.Identity, scale=-1.0, bias=epst[:, 0:1]
+            )
             rstd[key] = small.tile([P, 1], F32, name="rstd", tag="rstd", bufs=4)
-            nc.gpsimd.tensor_tensor(out=rstd[key][:], in0=u1[:], in1=mhalf[:], op=ALU.pow)
+            nc.gpsimd.tensor_tensor(out=rstd[key][:], in0=vareps[:], in1=mhalf[:], op=ALU.pow)
             if want_nb:
                 nbt[key] = small.tile([P, 1], F32, name="nb", tag="nb", bufs=2)
                 nc.gpsimd.tensor_tensor(out=nbt[key][:], in0=nm[:, 0:1], in1=rstd[key][:], op=ALU.mult)
 
+        early = [(j, h) for j in range(NJ - TAIL_NODES) for h in range(2)]
+        seq = early + [(j, h) for h in range(2) for j in range(NJ - TAIL_NODES, NJ)]
         trb = {}
         ge = {}
         ecs = {}
@@ -236,7 +251,7 @@ def tile_graphmodel_pa_t_kernel(tc, x, edge, WA, WB, WE, WU, WV, out_0, out_1):
         def t_transpose(t, tag="tr", bufs=1):
             if not ok(t):
                 return
-            j, h = t // 2, t % 2
+            j, h = seq[t]
             ef = ech[(h, j // 2)][:].bitcast(F32)
             trb[t] = transposes(ef[:, j % 2, :], tag, bufs)
 
@@ -258,12 +273,13 @@ def tile_graphmodel_pa_t_kernel(tc, x, edge, WA, WB, WE, WU, WV, out_0, out_1):
             )
             ecs[t] = (c_, s_)
 
-        def t_agg(t, n2):
+        def t_agg(t, n2, first=0, last=5):
             if not ok(t):
                 return
-            j, h = t // 2, t % 2
-            a_ = psum.tile([P, HALF], F32, name="acc", tag="acc", bufs=4)
-            acc[(t, n2)] = a_
+            j, h = seq[t]
+            if first == 0:
+                acc[(t, n2)] = psum.tile([P, HALF], F32, name="acc", tag="acc", bufs=4)
+            a_ = acc[(t, n2)]
             cols = slice(n2 * HALF, (n2 + 1) * HALF)
             c_, s_ = ecs[t]
             ops = [
@@ -274,7 +290,8 @@ def tile_graphmodel_pa_t_kernel(tc, x, edge, WA, WB, WE, WU, WV, out_0, out_1):
             i = 0
             for lc, ls, w in ops:
                 for g in range(2):
-                    mx(a_[:], lc[:, g, :], ls[:, g, :], wc[w][:, g, cols], ws[w][:, g, cols], i == 0, i == 5)
+                    if first <= i <= last:
+                        mx(a_[:], lc[:, g, :], ls[:, g, :], wc[w][:, g, cols], ws[w][:, g, cols], i == 0, i == 5)
                     i += 1
 
         def t_bn(t, n2):
@@ -297,6 +314,10 @@ def tile_graphmodel_pa_t_kernel(tc, x, edge, WA, WB, WE, WU, WV, out_0, out_1):
             if ok(t):
                 stats_out(t)
 
+        def t_negvar(t):
+            if ok(t):
+                stats_negvar(t)
+
         def t_rstd(t):
             if ok(t):
                 stats_rstd(t)
@@ -311,38 +332,41 @@ def tile_graphmodel_pa_t_kernel(tc, x, edge, WA, WB, WE, WU, WV, out_0, out_1):
                 out=rz[t][:, cols], in_=acc[(t, n2)][:], func=ACTF.Relu, bias=nmt[t][:, 0:1], scale=1.0
             )
 
-        def t_edge_out(t):
+        whole = slice(0, C)
+        halves = [slice(n2 * HALF, (n2 + 1) * HALF) for n2 in range(2)]
+
+        def t_edge_out(t, cols=whole):
             if not ok(t):
                 return
-            j, h = t // 2, t % 2
+            j, h = seq[t]
             nc.vector.scalar_tensor_tensor(
-                out=rz[t][:],
-                in0=rz[t][:],
+                out=rz[t][:, cols],
+                in0=rz[t][:, cols],
                 scalar=rstd[t][:, 0:1],
-                in1=ech[(h, j // 2)][:, j % 2, :],
+                in1=ech[(h, j // 2)][:, j % 2, cols],
                 op0=ALU.mult,
                 op1=ALU.add,
             )
-            nc.sync.dma_start(out=o1[h][:, j, :], in_=rz[t][:])
+            nc.sync.dma_start(out=o1[h][:, j, cols], in_=rz[t][:, cols])
 
-        def t_tanh(t):
+        def t_tanh(t, cols=whole):
             if not ok(t):
                 return
-            tet[t] = work.tile([P, C], F32, name="te", tag="te", bufs=3)
-            nc.scalar.activation(out=tet[t][:], in_=rz[t][:], func=ACTF.Tanh, scale=0.5)
+            if cols.start == 0:
+                tet[t] = work.tile([P, C], F32, name="te", tag="te", bufs=4)
+            nc.scalar.activation(out=tet[t][:, cols], in_=rz[t][:, cols], func=ACTF.Tanh, scale=0.5)
 
-        def t_exp(t):
+        def t_exp(t, cols=whole):
             if not ok(t):
                 return
-            j, h = t // 2, t % 2
+            j, h = seq[t]
             et[t] = den[h] if j == 0 else tet[t]
-            nc.scalar.activation(out=et[t][:], in_=tet[t][:], func=ACTF.Exp, scale=0.5)
-            if t == NT - 1:
-                nc.scalar.activation(out=warm2[:], in_=epst[:], func=ACTF.Ln)
+            nc.scalar.activation(out=et[t][:, cols], in_=tet[t][:, cols], func=ACTF.Exp, scale=0.5)
 
-        def u_node(j):
-            if not 0 <= j < NJ:
+        def t_u(t):
+            if not ok(t) or (t > 0 and seq[t - 1][0] == seq[t][0]):
                 return
+            j = seq[t][0]
             for n2 in range(2):
                 u_ = psum.tile([P, HALF], F32, name="ub", tag="ub", bufs=2)
                 cols = slice(n2 * HALF, (n2 + 1) * HALF)
@@ -353,23 +377,22 @@ def tile_graphmodel_pa_t_kernel(tc, x, edge, WA, WB, WE, WU, WV, out_0, out_1):
         def t_prod(t, n2):
             if not ok(t):
                 return
-            j, h = t // 2, t % 2
+            j, h = seq[t]
             if n2 == 0:
                 mt[t] = num[h] if j == 0 else work.tile([P, C], F32, name="mt", tag="mt", bufs=2)
             cols = slice(n2 * HALF, (n2 + 1) * HALF)
             nc.vector.tensor_tensor(out=mt[t][:, cols], in0=et[t][:, cols], in1=ubt[(j, n2)][:], op=ALU.mult)
 
-        def t_den(t):
-            if not ok(t) or t < 2:
+        def t_den(t, eng=nc.gpsimd, cols=whole):
+            if not ok(t) or seq[t][0] == 0:
                 return
-            h = t % 2
-            eng = nc.vector if t >= NT - 4 else nc.gpsimd
-            eng.tensor_tensor(out=den[h][:], in0=den[h][:], in1=et[t][:], op=ALU.add)
+            h = seq[t][1]
+            eng.tensor_tensor(out=den[h][:, cols], in0=den[h][:, cols], in1=et[t][:, cols], op=ALU.add)
 
         def t_num(t):
-            if not ok(t) or t < 2:
+            if not ok(t) or seq[t][0] == 0:
                 return
-            h = t % 2
+            h = seq[t][1]
             nc.vector.tensor_tensor(out=num[h][:], in0=num[h][:], in1=mt[t][:], op=ALU.add)
 
         start_tags = [("acc", 4), ("ub", 2)]
@@ -390,30 +413,30 @@ def tile_graphmodel_pa_t_kernel(tc, x, edge, WA, WB, WE, WU, WV, out_0, out_1):
                     )
                     t_transpose(0, "acc", 4)
                     t_regroup(0)
+                    t_transpose(1, "acc", 4)
+                    t_regroup(1)
                     for jj in range(4):
-                        xrep_copy(0, jj, False)
+                        for g in range(2):
+                            xrep_copy(0, jj, g, False)
                     t_quantise(0)
+                    t_quantise(1)
                     xrep_quant(0)
-                    t_transpose(2)
                 prep_w(w, 2 * n2, start_tags)
                 prep_w(w, 2 * n2 + 1, start_tags)
                 quant_w(w, n2)
-        load_e1(0, 1)
+        load_e(0, 1, 2)
+        load_w("WV", 0)
+        load_w("WV", 1)
         load_e(1)
-        for a in range(4):
-            load_w("WV", a)
+        load_w("WV", 2)
+        load_w("WV", 3)
         load_e(2)
 
-        uix = {}
+        for jj in range(4):
+            for g in range(2):
+                xrep_copy(1, jj, g, True)
 
-        def x_wu():
-            for h in range(2):
-                for n2 in range(2):
-                    u_ = psum.tile([P, HALF], F32, name="uix", tag="acc", bufs=4)
-                    cols = slice(n2 * HALF, (n2 + 1) * HALF)
-                    for g in range(2):
-                        mx(u_[:], xc[:, h, g, :], xs[:, h, g, :], wc["WU"][:, g, cols], ws["WU"][:, g, cols], g == 0, g == 1)
-                    uix[(h, n2)] = u_
+        uix = {}
 
         def wu_unit(k):
             u = (k - WU_FIRST_ROUND) // 2
@@ -422,145 +445,122 @@ def tile_graphmodel_pa_t_kernel(tc, x, edge, WA, WB, WE, WU, WV, out_0, out_1):
             return (u // 2, u % 2)
 
         for k in range(NT):
-            t_exp(k - 4)
-            t_regroup(k + 2)
+            t_exp(k - 3)
+            t_edge_out(k - 2)
+            if k in (2, 3):
+                xrep_quant(k)
             t_agg(k, 0)
             t_bn(k, 0)
+            t_agg(k, 1, 0, SPLIT - 1)
             t_sum(k - 1)
-            t_prod(k - 4, 0)
-            t_den(k - 4)
+            t_agg(k, 1, SPLIT, 5)
             t_out(k - 1)
+            if k > 0:
+                t_regroup(k + 3)
+            t_prod(k - 3, 0)
+            t_den(k - 4, nc.gpsimd, slice(0, DEN_POOL))
             t_relu(k - 1, 0)
-            t_agg(k, 1)
-            t_prod(k - 4, 1)
-            t_rstd(k - 1)
+            t_negvar(k - 1)
+            t_prod(k - 3, 1)
             t_relu(k - 1, 1)
+            t_rstd(k - 1)
             t_bn(k, 1)
+            if k > 0:
+                t_quantise(k + 2)
             t_aggr(k)
-            t_edge_out(k - 2)
-            t_e2(k)
-            if k in (1, 2):
-                quant_w("WV", k - 1)
-            if k in (WU_FIRST_ROUND + 8, WU_FIRST_ROUND + 16):
-                quant_w("WU", (k - WU_FIRST_ROUND) // 8 - 1)
-            t_transpose(k + 3)
-            if k % 2 == 1:
-                u_node((k - 3) // 2)
+            if k in (WU_FIRST_ROUND + 7, WU_FIRST_ROUND + 15):
+                quant_w("WU", (k - WU_FIRST_ROUND) // 8)
+            if k == 0:
+                t_transpose(2, "ub", 2)
+                t_transpose(3)
+                t_regroup(2)
+                t_regroup(3)
+                t_quantise(2)
+            wv = WV_UNITS[k] if k < 3 else ()
+            for i, u in enumerate(wv):
+                if u % 4 == 0:
+                    new_gw("WV", u // 4)
+                if i == 2:
+                    t_transpose(k + 4)
+                unit_t("WV", u // 2, u % 2, "ub", 2)
+                unit_r("WV", u // 2, u % 2, i == 0)
+                if u % 4 == 3:
+                    quant_w("WV", u // 4)
+            if len(wv) < 3:
+                t_transpose(k + 4)
+            t_u(k - 2)
             un = wu_unit(k)
             if un is not None:
                 if un[0] % 2 == 0 and un[1] == 0:
                     new_gw("WU", un[0] // 2)
                 unit_t("WU", un[0], un[1], "st", 1)
-            t_quantise(k + 2)
-            t_tanh(k - 3)
-            t_num(k - 4)
+            t_tanh(k - 2)
+            t_e2(k)
+            if k == 0:
+                xrep_quant(1)
+            for a, jj in XREP[k] if k < 3 else ():
+                for g in range(2):
+                    xrep_copy(a, jj, g, True)
             if un is not None:
                 unit_r("WU", un[0], un[1])
-            for a in (1, 2, 3):
-                if 8 * a - 7 <= k <= 8 * a - 4:
-                    xrep_copy(a, k - (8 * a - 7), True)
-                if k == 8 * a - 3:
-                    xrep_quant(a)
-            if k == 0:
-                t_transpose(1, "ub", 2)
-                t_regroup(1)
-                t_quantise(1)
-            if k < 2:
-                for u in range(4 * k, 4 * k + 4):
-                    if u % 4 == 0:
-                        new_gw("WV", u // 4)
-                    unit_t("WV", u // 2, u % 2, "ub", 2)
-                    unit_r("WV", u // 2, u % 2)
+            t_num(k - 3)
+            t_den(k - 3, nc.vector, slice(DEN_POOL, C))
             if k == 3:
                 for a in range(4):
                     load_w("WU", a)
             if k % 4 == 1 and 3 <= (k + 7) // 4 < NJ // 2:
                 load_e((k + 7) // 4)
 
-        t_exp(NT - 4)
-        t_sum(NT - 1)
-        t_edge_out(NT - 2)
-        t_tanh(NT - 3)
-        t_out(NT - 1)
-        t_relu(NT - 1, 0)
-        t_relu(NT - 1, 1)
-        t_rstd(NT - 1)
-        t_den(NT - 4)
-        t_prod(NT - 4, 0)
-        t_prod(NT - 4, 1)
-        t_exp(NT - 3)
-        t_num(NT - 4)
-        t_tanh(NT - 2)
-        t_edge_out(NT - 1)
-        t_den(NT - 3)
-        t_exp(NT - 2)
-        t_tanh(NT - 1)
-        t_den(NT - 2)
-        t_prod(NT - 3, 0)
-        t_prod(NT - 3, 1)
-        u_node(NJ - 1)
-        x_wu()
-        t_exp(NT - 1)
-        t_den(NT - 1)
-        t_num(NT - 3)
-        for t in (NT - 2, NT - 1):
-            t_prod(t, 0)
-            t_prod(t, 1)
-            t_num(t)
+        def x_wu(h, tag, bufs):
+            for n2 in range(2):
+                u_ = psum.tile([P, HALF], F32, name="uix", tag=tag, bufs=bufs)
+                cols = halves[n2]
+                for g in range(2):
+                    mx(u_[:], xc[:, h, g, :], xs[:, h, g, :], wc["WU"][:, g, cols], ws["WU"][:, g, cols], g == 0, g == 1)
+                uix[(h, n2)] = u_
 
-        units = [(h, n2) for h in range(2) for n2 in range(2)]
+        def recip(h):
+            for n2 in range(2):
+                nc.scalar.activation(
+                    out=den[h][:, halves[n2]], in_=den[h][:, halves[n2]], func=ACTF.Abs_reciprocal_sqrt, scale=16.0
+                )
+            for n2 in range(2):
+                cols = halves[n2]
+                nc.scalar.activation(out=den[h][:, cols], in_=den[h][:, cols], func=ACTF.Square)
+
         xnew = {}
-        for h in range(2):
-            xnew[h] = work.tile([P, C], F32, name="xnew", tag="rz", bufs=5)
-        for h, n2 in units:
-            cols = slice(n2 * HALF, (n2 + 1) * HALF)
-            nc.scalar.activation(out=den[h][:, cols], in_=den[h][:, cols], func=ACTF.Ln)
-        for h, n2 in units:
-            cols = slice(n2 * HALF, (n2 + 1) * HALF)
-            nc.scalar.activation(out=den[h][:, cols], in_=den[h][:, cols], func=ACTF.Exp, scale=-1.0)
 
         def tail_mul(h, n2):
-            cols = slice(n2 * HALF, (n2 + 1) * HALF)
-            eng = nc.gpsimd if h == 1 else nc.vector
-            eng.tensor_tensor(out=num[h][:, cols], in0=num[h][:, cols], in1=den[h][:, cols], op=ALU.mult)
+            cols = halves[n2]
+            nc.vector.tensor_tensor(out=num[h][:, cols], in0=num[h][:, cols], in1=den[h][:, cols], op=ALU.mult)
 
         def tail_add(h, n2):
-            cols = slice(n2 * HALF, (n2 + 1) * HALF)
-            nc.vector.scalar_tensor_tensor(
-                out=xnew[h][:, cols],
-                in0=num[h][:, cols],
-                scalar=1.0 / 16.0,
-                in1=uix[(h, n2)][:],
-                op0=ALU.mult,
-                op1=ALU.add,
-            )
+            cols = halves[n2]
+            if n2 == 0:
+                xnew[h] = work.tile([P, C], F32, name="xnew", tag="rz", bufs=5)
+            nc.vector.tensor_tensor(out=xnew[h][:, cols], in0=num[h][:, cols], in1=uix[(h, n2)][:], op=ALU.add)
 
         def tail_bn(h, n2):
-            cols = slice(n2 * HALF, (n2 + 1) * HALF)
-            stats_bn(("x", h), n2, xnew[h][:, cols])
+            stats_bn(("x", h), n2, xnew[h][:, halves[n2]])
 
-        for f in (tail_mul, tail_add, tail_bn):
-            f(0, 0)
-            f(0, 1)
-        tail_mul(1, 0)
-        stats_aggr(("x", 0))
-        tail_mul(1, 1)
-        stats_e2(("x", 0))
-        stats_sum(("x", 0))
-        stats_out(("x", 0))
-        stats_rstd(("x", 0), True)
-        for f in (tail_add, tail_bn):
-            f(1, 0)
-            f(1, 1)
-        stats_aggr(("x", 1))
-        stats_e2(("x", 1))
-        stats_sum(("x", 1))
-        stats_out(("x", 1))
-        stats_rstd(("x", 1), True)
-        for h in range(2):
+        def tail_x(h):
+            for f in (tail_mul, tail_add, tail_bn):
+                f(h, 0)
+                f(h, 1)
+
+        def tail_stats(h):
+            key = ("x", h)
+            stats_aggr(key)
+            stats_e2(key)
+            stats_sum(key)
+            stats_out(key)
+            stats_negvar(key)
+            stats_rstd(key, True)
+
+        def tail_out(h):
             key = ("x", h)
             for n2 in range(2):
-                cols = slice(n2 * HALF, (n2 + 1) * HALF)
+                cols = halves[n2]
                 nc.vector.scalar_tensor_tensor(
                     out=xnew[h][:, cols],
                     in0=xnew[h][:, cols],
@@ -573,3 +573,52 @@ def tile_graphmodel_pa_t_kernel(tc, x, edge, WA, WB, WE, WU, WV, out_0, out_1):
                     out=xnew[h][:, cols], in_=xnew[h][:, cols], func=ACTF.Relu, bias=nbt[key][:, 0:1], scale=1.0
                 )
                 nc.sync.dma_start(out=o0[h][:, cols], in_=xnew[h][:, cols])
+
+        t = NT - 1
+        t_exp(t - 2)
+        t_edge_out(t - 1)
+        t_sum(t)
+        t_out(t)
+        t_relu(t, 0)
+        t_negvar(t)
+        t_rstd(t)
+        t_relu(t, 1)
+        t_prod(t - 2, 0)
+        t_prod(t - 2, 1)
+        t_den(t - 3, nc.vector, slice(0, DEN_POOL))
+        t_num(t - 2)
+        t_u(t - 1)
+        t_tanh(t - 1)
+        t_exp(t - 1)
+        for cols in halves:
+            t_edge_out(t, cols)
+        t_den(t - 2, nc.vector)
+        x_wu(0, "acc", 4)
+        t_prod(t - 1, 0)
+        t_prod(t - 1, 1)
+        t_den(t - 1, nc.vector)
+        t_u(t)
+        for cols in halves:
+            t_tanh(t, cols)
+        for cols in halves:
+            t_exp(t, cols)
+        recip(0)
+        t_num(t - 1)
+        for cols in halves:
+            t_den(t, nc.vector, cols)
+        recip(1)
+        t_prod(t, 0)
+        t_prod(t, 1)
+        t_num(t)
+        x_wu(1, "acc", 4)
+        tail_x(0)
+        tail_mul(1, 0)
+        tail_mul(1, 1)
+        tail_stats(0)
+        tail_add(1, 0)
+        tail_add(1, 1)
+        tail_bn(1, 0)
+        tail_bn(1, 1)
+        tail_stats(1)
+        tail_out(0)
+        tail_out(1)

@@ -23,7 +23,7 @@ FLOPS = 2 * 1024 * 1024 * (4096 + 4 * 256)
 
 TAIL_NODES = 2
 XREP = (((2, 0), (2, 1), (2, 2)), ((2, 3), (3, 0), (3, 1)), ((3, 2), (3, 3)))
-DEN_POOL = 768
+DEN_POOL = 1024
 WV_UNITS = ((0, 1, 2), (3, 4, 5), (6, 7))
 WU_FIRST_ROUND = 9
 
@@ -389,6 +389,13 @@ def tile_graphmodel_pa_t_kernel(tc, x, edge, WA, WB, WE, WU, WV, out_0, out_1):
             h = seq[t][1]
             eng.tensor_tensor(out=den[h][:, cols], in0=den[h][:, cols], in1=et[t][:, cols], op=ALU.add)
 
+        gate = const.tile([P, 1], F32, name="gate")
+
+        def t_gate(t):
+            if not ok(t) or seq[t][0] == 0:
+                return
+            nc.vector.tensor_copy(out=gate[:], in_=den[seq[t][1]][:, 0:1])
+
         def t_num(t):
             if not ok(t) or seq[t][0] == 0:
                 return
@@ -446,11 +453,12 @@ def tile_graphmodel_pa_t_kernel(tc, x, edge, WA, WB, WE, WU, WV, out_0, out_1):
 
         for k in range(NT):
             t_exp(k - 3)
+            t_gate(k - 4)
             t_edge_out(k - 2)
-            if k in (2, 3):
-                xrep_quant(k)
             t_agg(k, 0)
             t_bn(k, 0)
+            if k == 3:
+                t_u(0)
             t_agg(k, 1, 0, SPLIT - 1)
             t_sum(k - 1)
             t_agg(k, 1, SPLIT, 5)
@@ -468,8 +476,6 @@ def tile_graphmodel_pa_t_kernel(tc, x, edge, WA, WB, WE, WU, WV, out_0, out_1):
             if k > 0:
                 t_quantise(k + 2)
             t_aggr(k)
-            if k in (WU_FIRST_ROUND + 7, WU_FIRST_ROUND + 15):
-                quant_w("WU", (k - WU_FIRST_ROUND) // 8)
             if k == 0:
                 t_transpose(2, "ub", 2)
                 t_transpose(3)
@@ -488,7 +494,8 @@ def tile_graphmodel_pa_t_kernel(tc, x, edge, WA, WB, WE, WU, WV, out_0, out_1):
                     quant_w("WV", u // 4)
             if len(wv) < 3:
                 t_transpose(k + 4)
-            t_u(k - 2)
+            if k != 2:
+                t_u(k - 2)
             un = wu_unit(k)
             if un is not None:
                 if un[0] % 2 == 0 and un[1] == 0:
@@ -496,15 +503,16 @@ def tile_graphmodel_pa_t_kernel(tc, x, edge, WA, WB, WE, WU, WV, out_0, out_1):
                 unit_t("WU", un[0], un[1], "st", 1)
             t_tanh(k - 2)
             t_e2(k)
-            if k == 0:
-                xrep_quant(1)
+            if k in (0, 2, 3):
+                xrep_quant(max(1, k))
             for a, jj in XREP[k] if k < 3 else ():
                 for g in range(2):
                     xrep_copy(a, jj, g, True)
             if un is not None:
                 unit_r("WU", un[0], un[1])
             t_num(k - 3)
-            t_den(k - 3, nc.vector, slice(DEN_POOL, C))
+            if k in (WU_FIRST_ROUND + 8, WU_FIRST_ROUND + 16):
+                quant_w("WU", (k - WU_FIRST_ROUND) // 8 - 1)
             if k == 3:
                 for a in range(4):
                     load_w("WU", a)
@@ -585,7 +593,7 @@ def tile_graphmodel_pa_t_kernel(tc, x, edge, WA, WB, WE, WU, WV, out_0, out_1):
         t_relu(t, 1)
         t_prod(t - 2, 0)
         t_prod(t - 2, 1)
-        t_den(t - 3, nc.vector, slice(0, DEN_POOL))
+        t_den(t - 3, nc.vector)
         t_num(t - 2)
         t_u(t - 1)
         t_tanh(t - 1)

@@ -389,13 +389,6 @@ def tile_graphmodel_pa_t_kernel(tc, x, edge, WA, WB, WE, WU, WV, out_0, out_1):
             h = seq[t][1]
             eng.tensor_tensor(out=den[h][:, cols], in0=den[h][:, cols], in1=et[t][:, cols], op=ALU.add)
 
-        gate = const.tile([P, 1], F32, name="gate")
-
-        def t_gate(t):
-            if not ok(t) or seq[t][0] == 0:
-                return
-            nc.vector.tensor_copy(out=gate[:], in_=den[seq[t][1]][:, 0:1])
-
         def t_num(t):
             if not ok(t) or seq[t][0] == 0:
                 return
@@ -453,7 +446,6 @@ def tile_graphmodel_pa_t_kernel(tc, x, edge, WA, WB, WE, WU, WV, out_0, out_1):
 
         for k in range(NT):
             t_exp(k - 3)
-            t_gate(k - 4)
             t_edge_out(k - 2)
             t_agg(k, 0)
             t_bn(k, 0)
@@ -466,7 +458,6 @@ def tile_graphmodel_pa_t_kernel(tc, x, edge, WA, WB, WE, WU, WV, out_0, out_1):
             if k > 0:
                 t_regroup(k + 3)
             t_prod(k - 3, 0)
-            t_den(k - 4, nc.gpsimd, slice(0, DEN_POOL))
             t_relu(k - 1, 0)
             t_negvar(k - 1)
             t_prod(k - 3, 1)
@@ -511,6 +502,7 @@ def tile_graphmodel_pa_t_kernel(tc, x, edge, WA, WB, WE, WU, WV, out_0, out_1):
             if un is not None:
                 unit_r("WU", un[0], un[1])
             t_num(k - 3)
+            t_den(k - 3, nc.vector)
             if k in (WU_FIRST_ROUND + 8, WU_FIRST_ROUND + 16):
                 quant_w("WU", (k - WU_FIRST_ROUND) // 8 - 1)
             if k == 3:
@@ -529,18 +521,27 @@ def tile_graphmodel_pa_t_kernel(tc, x, edge, WA, WB, WE, WU, WV, out_0, out_1):
 
         def recip(h):
             for n2 in range(2):
+                src = dn[n2][:] if h == 0 else den[h][:, halves[n2]]
                 nc.scalar.activation(
-                    out=den[h][:, halves[n2]], in_=den[h][:, halves[n2]], func=ACTF.Abs_reciprocal_sqrt, scale=16.0
+                    out=den[h][:, halves[n2]], in_=src, func=ACTF.Abs_reciprocal_sqrt, scale=16.0
                 )
             for n2 in range(2):
                 cols = halves[n2]
                 nc.scalar.activation(out=den[h][:, cols], in_=den[h][:, cols], func=ACTF.Square)
 
+        dn = []
+
+        def den_add(src, start, stop):
+            for n2 in range(2):
+                if start:
+                    dn.append(psum.tile([P, HALF], F32, name="dn", tag="acc", bufs=4))
+                nc.tensor.matmul(out=dn[n2][:], lhsT=ident[:], rhs=src[:, halves[n2]], start=start, stop=stop)
+
         xnew = {}
 
-        def tail_mul(h, n2):
+        def tail_mul(h, n2, eng=nc.vector):
             cols = halves[n2]
-            nc.vector.tensor_tensor(out=num[h][:, cols], in0=num[h][:, cols], in1=den[h][:, cols], op=ALU.mult)
+            eng.tensor_tensor(out=num[h][:, cols], in0=num[h][:, cols], in1=den[h][:, cols], op=ALU.mult)
 
         def tail_add(h, n2):
             cols = halves[n2]
@@ -556,31 +557,48 @@ def tile_graphmodel_pa_t_kernel(tc, x, edge, WA, WB, WE, WU, WV, out_0, out_1):
                 f(h, 0)
                 f(h, 1)
 
-        def tail_stats(h):
-            key = ("x", h)
-            stats_aggr(key)
-            stats_e2(key)
-            stats_sum(key)
-            stats_out(key)
-            stats_negvar(key)
-            stats_rstd(key, True)
+        def tail_e2(h):
+            mv = mvt[("x", h)]
+            nc.vector.tensor_scalar(
+                out=mv[:, 2:3], in0=mv[:, 0:1], scalar1=mv[:, 0:1], scalar2=mv[:, 1:2], op0=ALU.mult, op1=ALU.add
+            )
+            stats_sum(("x", h))
+            stats_out(("x", h))
 
-        def tail_out(h):
+        def tail_negvar(h):
             key = ("x", h)
-            for n2 in range(2):
-                cols = halves[n2]
-                nc.vector.scalar_tensor_tensor(
-                    out=xnew[h][:, cols],
-                    in0=xnew[h][:, cols],
-                    scalar=rstd[key][:, 0:1],
-                    in1=xn[:, h, cols],
-                    op0=ALU.mult,
-                    op1=ALU.add,
-                )
-                nc.scalar.activation(
-                    out=xnew[h][:, cols], in_=xnew[h][:, cols], func=ACTF.Relu, bias=nbt[key][:, 0:1], scale=1.0
-                )
-                nc.sync.dma_start(out=o0[h][:, cols], in_=xnew[h][:, cols])
+            st = pst[key]
+            negvar[key] = small.tile([P, 1], F32, name="negvarx", tag="negvarx", bufs=2)
+            nc.vector.tensor_scalar(
+                out=negvar[key][:], in0=st[:, 0:1], scalar1=st[:, 0:1], scalar2=st[:, 2:3], op0=ALU.mult, op1=ALU.add
+            )
+
+        def tail_rstd(h):
+            key = ("x", h)
+            vareps = small.tile([P, 1], F32, name="varepsx", tag="varepsx", bufs=2)
+            nc.vector.tensor_scalar(
+                out=vareps[:], in0=negvar[key][:], scalar1=-1.0, scalar2=EPS, op0=ALU.mult, op1=ALU.add
+            )
+            rstd[key] = small.tile([P, 1], F32, name="rstd", tag="rstd", bufs=4)
+            nc.gpsimd.tensor_tensor(out=rstd[key][:], in0=vareps[:], in1=mhalf[:], op=ALU.pow)
+            nbt[key] = small.tile([P, 1], F32, name="nb", tag="nb", bufs=2)
+            nc.gpsimd.tensor_tensor(out=nbt[key][:], in0=nmt[key][:, 0:1], in1=rstd[key][:], op=ALU.mult)
+
+        def tail_out(h, n2):
+            key = ("x", h)
+            cols = halves[n2]
+            nc.vector.scalar_tensor_tensor(
+                out=xnew[h][:, cols],
+                in0=xnew[h][:, cols],
+                scalar=rstd[key][:, 0:1],
+                in1=xn[:, h, cols],
+                op0=ALU.mult,
+                op1=ALU.add,
+            )
+            nc.scalar.activation(
+                out=xnew[h][:, cols], in_=xnew[h][:, cols], func=ACTF.Relu, bias=nbt[key][:, 0:1], scale=1.0
+            )
+            nc.sync.dma_start(out=o0[h][:, cols], in_=xnew[h][:, cols])
 
         t = NT - 1
         t_exp(t - 2)
@@ -593,14 +611,14 @@ def tile_graphmodel_pa_t_kernel(tc, x, edge, WA, WB, WE, WU, WV, out_0, out_1):
         t_relu(t, 1)
         t_prod(t - 2, 0)
         t_prod(t - 2, 1)
-        t_den(t - 3, nc.vector)
+        den_add(den[0], True, False)
         t_num(t - 2)
         t_u(t - 1)
+        den_add(et[t - 2], False, True)
         t_tanh(t - 1)
         t_exp(t - 1)
         for cols in halves:
             t_edge_out(t, cols)
-        t_den(t - 2, nc.vector)
         x_wu(0, "acc", 4)
         t_prod(t - 1, 0)
         t_prod(t - 1, 1)
@@ -620,13 +638,21 @@ def tile_graphmodel_pa_t_kernel(tc, x, edge, WA, WB, WE, WU, WV, out_0, out_1):
         t_num(t)
         x_wu(1, "acc", 4)
         tail_x(0)
-        tail_mul(1, 0)
-        tail_mul(1, 1)
-        tail_stats(0)
+        tail_mul(1, 0, nc.gpsimd)
+        tail_mul(1, 1, nc.gpsimd)
+        stats_aggr(("x", 0))
         tail_add(1, 0)
+        tail_e2(0)
         tail_add(1, 1)
         tail_bn(1, 0)
+        tail_negvar(0)
         tail_bn(1, 1)
-        tail_stats(1)
-        tail_out(0)
-        tail_out(1)
+        tail_rstd(0)
+        stats_aggr(("x", 1))
+        tail_e2(1)
+        tail_out(0, 0)
+        tail_negvar(1)
+        tail_rstd(1)
+        tail_out(0, 1)
+        tail_out(1, 0)
+        tail_out(1, 1)

@@ -23,9 +23,9 @@ FLOPS = 2 * 1024 * 1024 * (4096 + 4 * 256)
 
 TAIL_NODES = 2
 XREP = (((2, 0), (2, 1), (2, 2)), ((2, 3), (3, 0), (3, 1)), ((3, 2), (3, 3)))
-DEN_POOL = 1024
-WV_UNITS = ((0, 1, 2), (3, 4, 5), (6, 7))
-WU_FIRST_ROUND = 9
+DEN_POOL = 768
+WV_UNITS = ((0, 1), (2, 3), (4, 5), (6, 7))
+WU_FIRST_ROUND = 8
 
 
 def tile_graphmodel_pa_t_kernel(tc, x, edge, WA, WB, WE, WU, WV, out_0, out_1):
@@ -202,8 +202,8 @@ def tile_graphmodel_pa_t_kernel(tc, x, edge, WA, WB, WE, WU, WV, out_0, out_1):
 
         def stats_e2(key):
             mv = mvt[key]
-            nc.scalar.activation(
-                out=mv[:, 2:3], in_=mv[:, 0:1], func=ACTF.Identity, scale=mv[:, 0:1], bias=mv[:, 1:2]
+            nc.vector.tensor_scalar(
+                out=mv[:, 2:3], in0=mv[:, 0:1], scalar1=mv[:, 0:1], scalar2=mv[:, 1:2], op0=ALU.mult, op1=ALU.add
             )
 
         def stats_sum(key):
@@ -220,18 +220,6 @@ def tile_graphmodel_pa_t_kernel(tc, x, edge, WA, WB, WE, WU, WV, out_0, out_1):
             nc.scalar.activation(
                 out=negvar[key][:], in_=nm[:, 0:1], func=ACTF.Identity, scale=nm[:, 0:1], bias=nm[:, 2:3]
             )
-
-        def stats_rstd(key, want_nb=False):
-            nm = nmt[key]
-            vareps = small.tile([P, 1], F32, name="vareps", tag="vareps", bufs=3)
-            nc.scalar.activation(
-                out=vareps[:], in_=negvar[key][:], func=ACTF.Identity, scale=-1.0, bias=epst[:, 0:1]
-            )
-            rstd[key] = small.tile([P, 1], F32, name="rstd", tag="rstd", bufs=4)
-            nc.gpsimd.tensor_tensor(out=rstd[key][:], in0=vareps[:], in1=mhalf[:], op=ALU.pow)
-            if want_nb:
-                nbt[key] = small.tile([P, 1], F32, name="nb", tag="nb", bufs=2)
-                nc.gpsimd.tensor_tensor(out=nbt[key][:], in0=nm[:, 0:1], in1=rstd[key][:], op=ALU.mult)
 
         early = [(j, h) for j in range(NJ - TAIL_NODES) for h in range(2)]
         seq = early + [(j, h) for h in range(2) for j in range(NJ - TAIL_NODES, NJ)]
@@ -318,9 +306,21 @@ def tile_graphmodel_pa_t_kernel(tc, x, edge, WA, WB, WE, WU, WV, out_0, out_1):
             if ok(t):
                 stats_negvar(t)
 
+        vareps = {}
+
+        def t_vareps(t):
+            if not ok(t):
+                return
+            vareps[t] = small.tile([P, 1], F32, name="vareps", tag="vareps", bufs=3)
+            nc.vector.tensor_scalar(
+                out=vareps[t][:], in0=negvar[t][:], scalar1=-1.0, scalar2=EPS, op0=ALU.mult, op1=ALU.add
+            )
+
         def t_rstd(t):
-            if ok(t):
-                stats_rstd(t)
+            if not ok(t):
+                return
+            rstd[t] = small.tile([P, 1], F32, name="rstd", tag="rstd", bufs=4)
+            nc.gpsimd.tensor_tensor(out=rstd[t][:], in0=vareps[t][:], in1=mhalf[:], op=ALU.pow)
 
         def t_relu(t, n2):
             if not ok(t):
@@ -353,7 +353,7 @@ def tile_graphmodel_pa_t_kernel(tc, x, edge, WA, WB, WE, WU, WV, out_0, out_1):
             if not ok(t):
                 return
             if cols.start == 0:
-                tet[t] = work.tile([P, C], F32, name="te", tag="te", bufs=4)
+                tet[t] = work.tile([P, C], F32, name="te", tag="te", bufs=3)
             nc.scalar.activation(out=tet[t][:, cols], in_=rz[t][:, cols], func=ACTF.Tanh, scale=0.5)
 
         def t_exp(t, cols=whole):
@@ -445,24 +445,25 @@ def tile_graphmodel_pa_t_kernel(tc, x, edge, WA, WB, WE, WU, WV, out_0, out_1):
             return (u // 2, u % 2)
 
         for k in range(NT):
-            t_exp(k - 3)
-            t_edge_out(k - 2)
+            if k > 0:
+                t_regroup(k + 3)
+            t_tanh(k - 3)
             t_agg(k, 0)
             t_bn(k, 0)
-            if k == 3:
+            if k == 4:
                 t_u(0)
             t_agg(k, 1, 0, SPLIT - 1)
             t_sum(k - 1)
             t_agg(k, 1, SPLIT, 5)
             t_out(k - 1)
-            if k > 0:
-                t_regroup(k + 3)
-            t_prod(k - 3, 0)
+            t_rstd(k - 2)
+            t_den(k - 4, nc.gpsimd, slice(0, DEN_POOL))
+            t_prod(k - 4, 0)
             t_relu(k - 1, 0)
             t_negvar(k - 1)
-            t_prod(k - 3, 1)
+            t_prod(k - 4, 1)
             t_relu(k - 1, 1)
-            t_rstd(k - 1)
+            t_exp(k - 3)
             t_bn(k, 1)
             if k > 0:
                 t_quantise(k + 2)
@@ -473,7 +474,7 @@ def tile_graphmodel_pa_t_kernel(tc, x, edge, WA, WB, WE, WU, WV, out_0, out_1):
                 t_regroup(2)
                 t_regroup(3)
                 t_quantise(2)
-            wv = WV_UNITS[k] if k < 3 else ()
+            wv = WV_UNITS[k] if k < len(WV_UNITS) else ()
             for i, u in enumerate(wv):
                 if u % 4 == 0:
                     new_gw("WV", u // 4)
@@ -485,27 +486,30 @@ def tile_graphmodel_pa_t_kernel(tc, x, edge, WA, WB, WE, WU, WV, out_0, out_1):
                     quant_w("WV", u // 4)
             if len(wv) < 3:
                 t_transpose(k + 4)
-            if k != 2:
-                t_u(k - 2)
+            if k != 3:
+                t_u(k - 3)
             un = wu_unit(k)
             if un is not None:
                 if un[0] % 2 == 0 and un[1] == 0:
                     new_gw("WU", un[0] // 2)
                 unit_t("WU", un[0], un[1], "st", 1)
-            t_tanh(k - 2)
+            t_num(k - 4)
+            t_den(k - 4, nc.vector, slice(DEN_POOL, C))
             t_e2(k)
-            if k in (0, 2, 3):
-                xrep_quant(max(1, k))
+            t_vareps(k - 1)
+            t_edge_out(k - 2)
+            if k == 0:
+                xrep_quant(1)
             for a, jj in XREP[k] if k < 3 else ():
                 for g in range(2):
                     xrep_copy(a, jj, g, True)
+            if k in (2, 3):
+                xrep_quant(k)
             if un is not None:
                 unit_r("WU", un[0], un[1])
-            t_num(k - 3)
-            t_den(k - 3, nc.vector)
             if k in (WU_FIRST_ROUND + 8, WU_FIRST_ROUND + 16):
                 quant_w("WU", (k - WU_FIRST_ROUND) // 8 - 1)
-            if k == 3:
+            if k == 4:
                 for a in range(4):
                     load_w("WU", a)
             if k % 4 == 1 and 3 <= (k + 7) // 4 < NJ // 2:
@@ -575,12 +579,12 @@ def tile_graphmodel_pa_t_kernel(tc, x, edge, WA, WB, WE, WU, WV, out_0, out_1):
 
         def tail_rstd(h):
             key = ("x", h)
-            vareps = small.tile([P, 1], F32, name="varepsx", tag="varepsx", bufs=2)
+            varepsx = small.tile([P, 1], F32, name="varepsx", tag="varepsx", bufs=2)
             nc.vector.tensor_scalar(
-                out=vareps[:], in0=negvar[key][:], scalar1=-1.0, scalar2=EPS, op0=ALU.mult, op1=ALU.add
+                out=varepsx[:], in0=negvar[key][:], scalar1=-1.0, scalar2=EPS, op0=ALU.mult, op1=ALU.add
             )
             rstd[key] = small.tile([P, 1], F32, name="rstd", tag="rstd", bufs=4)
-            nc.gpsimd.tensor_tensor(out=rstd[key][:], in0=vareps[:], in1=mhalf[:], op=ALU.pow)
+            nc.gpsimd.tensor_tensor(out=rstd[key][:], in0=varepsx[:], in1=mhalf[:], op=ALU.pow)
             nbt[key] = small.tile([P, 1], F32, name="nb", tag="nb", bufs=2)
             nc.gpsimd.tensor_tensor(out=nbt[key][:], in0=nmt[key][:, 0:1], in1=rstd[key][:], op=ALU.mult)
 
@@ -601,24 +605,32 @@ def tile_graphmodel_pa_t_kernel(tc, x, edge, WA, WB, WE, WU, WV, out_0, out_1):
             nc.sync.dma_start(out=o0[h][:, cols], in_=xnew[h][:, cols])
 
         t = NT - 1
-        t_exp(t - 2)
-        t_edge_out(t - 1)
+        t_tanh(t - 2)
         t_sum(t)
+        t_prod(t - 3, 0)
+        t_prod(t - 3, 1)
+        t_rstd(t - 1)
+        t_u(t - 2)
+        den_add(den[0], True, False)
+        den_add(et[t - 3], False, False)
         t_out(t)
         t_relu(t, 0)
         t_negvar(t)
-        t_rstd(t)
         t_relu(t, 1)
+        t_exp(t - 2)
+        t_num(t - 3)
+        t_vareps(t)
+        t_rstd(t)
+        t_edge_out(t - 1)
         t_prod(t - 2, 0)
         t_prod(t - 2, 1)
-        den_add(den[0], True, False)
-        t_num(t - 2)
         t_u(t - 1)
         den_add(et[t - 2], False, True)
         t_tanh(t - 1)
         t_exp(t - 1)
         for cols in halves:
             t_edge_out(t, cols)
+        t_num(t - 2)
         x_wu(0, "acc", 4)
         t_prod(t - 1, 0)
         t_prod(t - 1, 1)

@@ -21,7 +21,7 @@ EPS = 1e-5
 SPLIT = 2
 FLOPS = 2 * 1024 * 1024 * (4096 + 4 * 256)
 
-TAIL_NODES = 2
+TAIL_NODES = 1
 XREP = (((2, 0), (2, 1), (2, 2)), ((2, 3), (3, 0), (3, 1)), ((3, 2), (3, 3)))
 DEN_POOL = 768
 WV_UNITS = ((0, 1), (2, 3), (4, 5), (6, 7))
@@ -84,12 +84,12 @@ def tile_graphmodel_pa_t_kernel(tc, x, edge, WA, WB, WE, WU, WV, out_0, out_1):
         den = [const.tile([P, C], F32, name="den%d" % h) for h in range(2)]
         num = [const.tile([P, C], F32, name="num%d" % h) for h in range(2)]
 
-        def transposes(src_f32, tag, bufs):
+        def transposes(src_f32, tag, bufs, sorted_words=False):
             bank = psum.tile([P, HALF], F32, name="bank_" + tag, tag=tag, bufs=bufs)
             for g in range(2):
                 for u in range(2):
                     cols = slice((2 * g + u) * P, (2 * g + u + 1) * P)
-                    words = src_f32[:, 256 * g + u : 256 * (g + 1) : 2]
+                    words = src_f32[:, cols] if sorted_words else src_f32[:, 256 * g + u : 256 * (g + 1) : 2]
                     nc.tensor.transpose(bank[:, cols], words, ident[:])
             return bank
 
@@ -133,8 +133,20 @@ def tile_graphmodel_pa_t_kernel(tc, x, edge, WA, WB, WE, WU, WV, out_0, out_1):
         gwt = {}
         ubank = {}
 
+        wp = {}
+
+        def unit_p(w, a, r2):
+            wp[(w, a, r2)] = stage.tile([P, 512], F32, name="wp", tag="wp", bufs=2)
+            nc.vector.tensor_copy(
+                out=wp[(w, a, r2)][:].rearrange("p (g u q) -> p g u q", g=2, u=2),
+                in_=wn[(w, a)][:].bitcast(F32)[:, r2, :].rearrange("p (g q u) -> p g u q", g=2, u=2),
+            )
+
         def unit_t(w, a, r2, tag, bufs):
-            ubank[(w, a, r2)] = transposes(wn[(w, a)][:].bitcast(F32)[:, r2, :], tag, bufs)
+            if (w, a, r2) in wp:
+                ubank[(w, a, r2)] = transposes(wp[(w, a, r2)], tag, bufs, True)
+            else:
+                ubank[(w, a, r2)] = transposes(wn[(w, a)][:].bitcast(F32)[:, r2, :], tag, bufs)
 
         def unit_r(w, a, r2, on_vector=False):
             gwf = gwt[(w, a // 2)][:].bitcast(F32).rearrange("q g (r u) -> q g r u", u=2)
@@ -202,8 +214,8 @@ def tile_graphmodel_pa_t_kernel(tc, x, edge, WA, WB, WE, WU, WV, out_0, out_1):
 
         def stats_e2(key):
             mv = mvt[key]
-            nc.vector.tensor_scalar(
-                out=mv[:, 2:3], in0=mv[:, 0:1], scalar1=mv[:, 0:1], scalar2=mv[:, 1:2], op0=ALU.mult, op1=ALU.add
+            nc.scalar.activation(
+                out=mv[:, 2:3], in_=mv[:, 0:1], func=ACTF.Identity, scale=mv[:, 0:1], bias=mv[:, 1:2]
             )
 
         def stats_sum(key):
@@ -448,6 +460,9 @@ def tile_graphmodel_pa_t_kernel(tc, x, edge, WA, WB, WE, WU, WV, out_0, out_1):
             if k > 0:
                 t_regroup(k + 3)
             t_tanh(k - 3)
+            wv = WV_UNITS[k] if k < len(WV_UNITS) else ()
+            for u in wv:
+                unit_p("WV", u // 2, u % 2)
             t_agg(k, 0)
             t_bn(k, 0)
             if k == 4:
@@ -474,14 +489,13 @@ def tile_graphmodel_pa_t_kernel(tc, x, edge, WA, WB, WE, WU, WV, out_0, out_1):
                 t_regroup(2)
                 t_regroup(3)
                 t_quantise(2)
-            wv = WV_UNITS[k] if k < len(WV_UNITS) else ()
             for i, u in enumerate(wv):
                 if u % 4 == 0:
                     new_gw("WV", u // 4)
                 if i == 2:
                     t_transpose(k + 4)
                 unit_t("WV", u // 2, u % 2, "ub", 2)
-                unit_r("WV", u // 2, u % 2, i == 0)
+                unit_r("WV", u // 2, u % 2, i == 0 or k == 3)
                 if u % 4 == 3:
                     quant_w("WV", u // 4)
             if len(wv) < 3:
@@ -515,8 +529,9 @@ def tile_graphmodel_pa_t_kernel(tc, x, edge, WA, WB, WE, WU, WV, out_0, out_1):
             if k % 4 == 1 and 3 <= (k + 7) // 4 < NJ // 2:
                 load_e((k + 7) // 4)
 
-        def x_wu(h, tag, bufs):
+        def x_wu(h, tags):
             for n2 in range(2):
+                tag, bufs = tags[n2]
                 u_ = psum.tile([P, HALF], F32, name="uix", tag=tag, bufs=bufs)
                 cols = halves[n2]
                 for g in range(2):
@@ -525,21 +540,20 @@ def tile_graphmodel_pa_t_kernel(tc, x, edge, WA, WB, WE, WU, WV, out_0, out_1):
 
         def recip(h):
             for n2 in range(2):
-                src = dn[n2][:] if h == 0 else den[h][:, halves[n2]]
                 nc.scalar.activation(
-                    out=den[h][:, halves[n2]], in_=src, func=ACTF.Abs_reciprocal_sqrt, scale=16.0
+                    out=den[h][:, halves[n2]], in_=dn[(h, n2)][:], func=ACTF.Abs_reciprocal_sqrt, scale=16.0
                 )
             for n2 in range(2):
                 cols = halves[n2]
                 nc.scalar.activation(out=den[h][:, cols], in_=den[h][:, cols], func=ACTF.Square)
 
-        dn = []
+        dn = {}
 
-        def den_add(src, start, stop):
+        def den_add(h, src, start, stop):
             for n2 in range(2):
                 if start:
-                    dn.append(psum.tile([P, HALF], F32, name="dn", tag="acc", bufs=4))
-                nc.tensor.matmul(out=dn[n2][:], lhsT=ident[:], rhs=src[:, halves[n2]], start=start, stop=stop)
+                    dn[(h, n2)] = psum.tile([P, HALF], F32, name="dn", tag="acc", bufs=4)
+                nc.tensor.matmul(out=dn[(h, n2)][:], lhsT=ident[:], rhs=src[:, halves[n2]], start=start, stop=stop)
 
         xnew = {}
 
@@ -610,9 +624,8 @@ def tile_graphmodel_pa_t_kernel(tc, x, edge, WA, WB, WE, WU, WV, out_0, out_1):
         t_prod(t - 3, 0)
         t_prod(t - 3, 1)
         t_rstd(t - 1)
-        t_u(t - 2)
-        den_add(den[0], True, False)
-        den_add(et[t - 3], False, False)
+        den_add(0, den[0], True, False)
+        den_add(0, et[t - 3], False, False)
         t_out(t)
         t_relu(t, 0)
         t_negvar(t)
@@ -624,31 +637,30 @@ def tile_graphmodel_pa_t_kernel(tc, x, edge, WA, WB, WE, WU, WV, out_0, out_1):
         t_edge_out(t - 1)
         t_prod(t - 2, 0)
         t_prod(t - 2, 1)
+        den_add(1, den[1], True, False)
         t_u(t - 1)
-        den_add(et[t - 2], False, True)
         t_tanh(t - 1)
         t_exp(t - 1)
         for cols in halves:
             t_edge_out(t, cols)
         t_num(t - 2)
-        x_wu(0, "acc", 4)
+        den_add(0, et[t - 1], False, True)
+        den_add(1, et[t - 2], False, False)
         t_prod(t - 1, 0)
         t_prod(t - 1, 1)
-        t_den(t - 1, nc.vector)
-        t_u(t)
         for cols in halves:
             t_tanh(t, cols)
         for cols in halves:
             t_exp(t, cols)
+        den_add(1, et[t], False, True)
         recip(0)
         t_num(t - 1)
-        for cols in halves:
-            t_den(t, nc.vector, cols)
         recip(1)
         t_prod(t, 0)
         t_prod(t, 1)
+        x_wu(0, [("tr", 1), ("ub", 2)])
         t_num(t)
-        x_wu(1, "acc", 4)
+        x_wu(1, [("acc", 4), ("acc", 4)])
         tail_x(0)
         tail_mul(1, 0, nc.gpsimd)
         tail_mul(1, 1, nc.gpsimd)

@@ -248,12 +248,27 @@ def tile_graphmodel_pa_t_kernel(tc, x, edge, WA, WB, WE, WU, WV, out_0, out_1):
         def ok(t):
             return 0 <= t < NT
 
+        esort = {}
+
+        def t_sort(t):
+            if not ok(t):
+                return
+            j, h = t // 2, t % 2
+            esort[t] = stage.tile([P, 512], F32, name="esort", tag="esort", bufs=2)
+            nc.scalar.copy(
+                out=esort[t][:].rearrange("p (g u q) -> p g u q", g=2, u=2),
+                in_=ech[(h, j // 2)][:].bitcast(F32)[:, j % 2, :].rearrange("p (g q u) -> p g u q", g=2, u=2),
+            )
+
         def t_transpose(t, tag="tr", bufs=1):
             if not ok(t):
                 return
             j, h = seq[t]
             ef = ech[(h, j // 2)][:].bitcast(F32)
-            trb[t] = transposes(ef[:, j % 2, :], tag, bufs)
+            if t in esort:
+                trb[t] = transposes(esort[t], tag, bufs, True)
+            else:
+                trb[t] = transposes(ef[:, j % 2, :], tag, bufs)
 
         def t_regroup(t):
             if not ok(t):
@@ -521,6 +536,8 @@ def tile_graphmodel_pa_t_kernel(tc, x, edge, WA, WB, WE, WU, WV, out_0, out_1):
                 xrep_quant(k)
             if un is not None:
                 unit_r("WU", un[0], un[1])
+            if k > 1 and un is None:
+                t_sort(k + 5)
             if k in (WU_FIRST_ROUND + 8, WU_FIRST_ROUND + 16):
                 quant_w("WU", (k - WU_FIRST_ROUND) // 8 - 1)
             if k == 4:

from contextlib import ExitStack

import concourse.mybir as mybir
from concourse.masks import make_identity

F32 = mybir.dt.float32
BF16 = mybir.dt.bfloat16
U32 = mybir.dt.uint32
U8 = mybir.dt.uint8
FP8X4 = mybir.dt.float8_e4m3fn_x4
ALU = mybir.AluOpType
ACTF = mybir.ActivationFunctionType
AX = mybir.AxisListType

P = 128
C = 1024
NJ = 16
NT = 32
HALF = 512
EPS = 1e-5
SPLIT = 2
FLOPS = 2 * 1024 * 1024 * (4096 + 4 * 256)

TAIL_NODES = 1
XREP = (((2, 0), (2, 1), (2, 2)), ((2, 3), (3, 0), (3, 1)), ((3, 2), (3, 3)))
DEN_POOL = 768
WV_UNITS = ((0, 1), (2, 3), (4, 5), (6, 7))
WU_FIRST_ROUND = 8


def tile_graphmodel_pa_t_kernel(tc, x, edge, WA, WB, WE, WU, WV, out_0, out_1):
    nc = tc.nc
    with ExitStack() as ctx:
        const = ctx.enter_context(tc.tile_pool(name="const", bufs=1))
        stage = ctx.enter_context(tc.tile_pool(name="stage", bufs=2))
        work = ctx.enter_context(tc.tile_pool(name="work", bufs=2))
        small = ctx.enter_context(tc.tile_pool(name="small", bufs=3))
        psum = ctx.enter_context(tc.psum_pool(name="psum", bufs=1))
        ctx.enter_context(tc.manual_schedule())

        xv = x.flatten_outer_dims().rearrange("(p h) c -> h p c", h=2)
        o0 = out_0.flatten_outer_dims().rearrange("(p h) c -> h p c", h=2)
        ev = edge.flatten_outer_dims().rearrange("(p h j) c -> h p j c", h=2, j=NJ)
        o1 = out_1.flatten_outer_dims().rearrange("(p h j) c -> h p j c", h=2, j=NJ)
        wdram = {"WA": WA, "WB": WB, "WE": WE, "WU": WU, "WV": WV}
        wview = {}
        for w in wdram:
            wview[w] = wdram[w].rearrange("(a r p) k -> a p r k", a=4, r=2)

        warm = const.tile([P, 1], F32, name="warm")
        nc.vector.memset(warm[:], 0.0)
        warm2 = const.tile([P, 1], F32, name="warm2")
        nc.scalar.activation(out=warm2[:], in_=warm[:], func=ACTF.Exp)
        mhalf = const.tile([P, 1], F32, name="mhalf")
        nc.vector.memset(mhalf[:], -0.5)
        epst = const.tile([P, 1], F32, name="epst")
        nc.vector.memset(epst[:], EPS)
        ident = const.tile([P, P], F32, name="ident")
        make_identity(nc, ident[:])
        rsel = const.tile([P, 8], F32, name="rsel")
        nc.vector.tensor_reduce(
            out=rsel[:], in_=ident[:].rearrange("p (a r) -> p r a", r=8), axis=AX.X, op=ALU.add
        )
        negg = const.tile([P, P], F32, name="negg")
        nc.vector.tensor_scalar(
            out=negg[:].rearrange("p (a r) -> p a r", r=8),
            in0=rsel[:].unsqueeze(1).to_broadcast([P, 16, 8]),
            scalar1=-1.0 / 16.0,
            scalar2=None,
            op0=ALU.mult,
        )

        wc = {}
        ws = {}
        for w in wdram:
            wc[w] = const.tile([P, 2, C], U32, name="wc" + w, align_bytes=64)
            ws[w] = const.tile([P, 2, C], U8, name="ws" + w, align_bytes=64)
        xn = const.tile([P, 2, C], BF16, name="xn")
        gx = const.tile([P, 2, 2, 512], BF16, name="gx", align_bytes=64)
        xc = const.tile([P, 2, 2, P], U32, name="xc", align_bytes=64)
        xs = const.tile([P, 2, 2, P], U8, name="xs", align_bytes=64)
        xrc = const.tile([P, NJ, 2, P], U32, name="xrc", align_bytes=64)
        xrs = const.tile([P, NJ, 2, P], U8, name="xrs", align_bytes=64)
        den = [const.tile([P, C], F32, name="den%d" % h) for h in range(2)]
        num = [const.tile([P, C], F32, name="num%d" % h) for h in range(2)]

        def transposes(src_f32, tag, bufs, sorted_words=False):
            bank = psum.tile([P, HALF], F32, name="bank_" + tag, tag=tag, bufs=bufs)
            for g in range(2):
                for u in range(2):
                    cols = slice((2 * g + u) * P, (2 * g + u + 1) * P)
                    words = src_f32[:, cols] if sorted_words else src_f32[:, 256 * g + u : 256 * (g + 1) : 2]
                    nc.tensor.transpose(bank[:, cols], words, ident[:])
            return bank

        def regroup(dst_f32, bank, on_vector=False):
            src = bank[:].rearrange("q (g u r) -> q g r u", g=2, u=2)
            if on_vector:
                nc.vector.tensor_copy(out=dst_f32, in_=src)
            else:
                nc.scalar.copy(out=dst_f32, in_=src)

        def mx(out, lc, ls, rc, rs, start, stop):
            nc.tensor.matmul_mx(
                out=out,
                lhsT=lc.bitcast(FP8X4),
                lhsT_scale=ls,
                rhs=rc.bitcast(FP8X4),
                rhs_scale=rs,
                start=start,
                stop=stop,
            )

        wn = {}

        def load_w(w, a):
            t = stage.tile([P, 2, C], BF16, name="wn", tag="wn", bufs=4)
            nc.sync.dma_start(out=t[:], in_=wview[w][a])
            wn[(w, a)] = t

        ech = {}

        def load_e(jc, j0=0, j1=2):
            for h in range(2):
                if j0 == 0:
                    ech[(h, jc)] = stage.tile([P, 2, C], BF16, name="ech", tag="ech", bufs=6)
                nc.sync.dma_start(out=ech[(h, jc)][:, j0:j1, :], in_=ev[h][:, 2 * jc + j0 : 2 * jc + j1, :])

        for h in range(2):
            nc.sync.dma_start(out=xn[:, h, :], in_=xv[h])
        load_e(0, 0, 1)

        gwt = {}
        ubank = {}

        wp = {}

        def unit_p(w, a, r2):
            wp[(w, a, r2)] = stage.tile([P, 512], F32, name="wp", tag="wp", bufs=2)
            nc.vector.tensor_copy(
                out=wp[(w, a, r2)][:].rearrange("p (g u q) -> p g u q", g=2, u=2),
                in_=wn[(w, a)][:].bitcast(F32)[:, r2, :].rearrange("p (g q u) -> p g u q", g=2, u=2),
            )

        def unit_t(w, a, r2, tag, bufs):
            if (w, a, r2) in wp:
                ubank[(w, a, r2)] = transposes(wp[(w, a, r2)], tag, bufs, True)
            else:
                ubank[(w, a, r2)] = transposes(wn[(w, a)][:].bitcast(F32)[:, r2, :], tag, bufs)

        def unit_r(w, a, r2, on_vector=False):
            gwf = gwt[(w, a // 2)][:].bitcast(F32).rearrange("q g (r u) -> q g r u", u=2)
            r0 = ((a % 2) * 2 + r2) * P
            regroup(gwf[:, :, r0 : r0 + P, :], ubank[(w, a, r2)], on_vector)

        def new_gw(w, n2):
            gwt[(w, n2)] = stage.tile([P, 2, 2048], BF16, name="gw", tag="gw", bufs=3, align_bytes=64)

        def prep_w(w, a, tags):
            if a % 2 == 0:
                new_gw(w, a // 2)
            for r2 in range(2):
                tag, bufs = tags[r2 % len(tags)]
                unit_t(w, a, r2, tag, bufs)
                unit_r(w, a, r2, w == "WB" and a == 3 and r2 == 1)

        def quant_w(w, n2):
            cols = slice(n2 * HALF, (n2 + 1) * HALF)
            for g in range(2):
                nc.vector.quantize_mx(
                    out=wc[w][:, g, cols].bitcast(FP8X4),
                    scales=ws[w][:, g, cols],
                    in_=gwt[(w, n2)][:, g, :],
                )

        grxt = {}

        def xrep_copy(a, jj, g, on_scalar):
            if jj == 0 and g == 0:
                grxt[a] = stage.tile([P, 4, 2, 512], BF16, name="grx", tag="gw", bufs=3, align_bytes=64)
            grf = grxt[a][:].bitcast(F32)
            gxf = gx[:].bitcast(F32)
            j = 4 * a + jj
            src = gxf[:, j % 2, g, :].rearrange("q (b l u) -> q b l u", b=16, l=8)[:, :, j // 2, :]
            dst = grf[:, jj, g, :].rearrange("q (b i u) -> q b i u", b=16, i=8)
            if on_scalar:
                nc.scalar.copy(out=dst, in_=src.unsqueeze(2).to_broadcast([P, 16, 8, 2]))
            else:
                nc.vector.tensor_copy(out=dst, in_=src.unsqueeze(2).to_broadcast([P, 16, 8, 2]))

        def xrep_quant(a):
            nc.vector.quantize_mx(
                out=xrc[:, 4 * a : 4 * a + 4, :, :].rearrange("q j g r -> q (j g r)").bitcast(FP8X4),
                scales=xrs[:, 4 * a : 4 * a + 4, :, :].rearrange("q j g r -> q (j g r)"),
                in_=grxt[a][:].rearrange("q j g w -> q (j g w)"),
            )

        bstt = {}
        mvt = {}
        pst = {}
        nmt = {}
        negvar = {}
        rstd = {}
        nbt = {}

        def stats_bn(key, n2, src):
            if n2 == 0:
                bstt[key] = small.tile([P, 12], F32, name="bst", tag="bst", bufs=3)
            nc.vector.bn_stats(out=bstt[key][:, 6 * n2 : 6 * n2 + 6], in_=src)

        def stats_aggr(key):
            mvt[key] = small.tile([P, 3], F32, name="mv", tag="mv", bufs=3)
            nc.vector.bn_aggr(out=mvt[key][:, 0:2], in_=bstt[key][:])

        def stats_e2(key):
            mv = mvt[key]
            nc.scalar.activation(
                out=mv[:, 2:3], in_=mv[:, 0:1], func=ACTF.Identity, scale=mv[:, 0:1], bias=mv[:, 1:2]
            )

        def stats_sum(key):
            pst[key] = psum.tile([P, HALF], F32, name="st", tag="st", bufs=1)
            nc.tensor.matmul(out=pst[key][:, 0:3], lhsT=negg[:], rhs=mvt[key][:], start=True, stop=True)

        def stats_out(key):
            nmt[key] = small.tile([P, 3], F32, name="nm", tag="nm", bufs=4)
            nc.scalar.copy(out=nmt[key][:], in_=pst[key][:, 0:3])

        def stats_negvar(key):
            nm = nmt[key]
            negvar[key] = small.tile([P, 1], F32, name="negvar", tag="negvar", bufs=3)
            nc.scalar.activation(
                out=negvar[key][:], in_=nm[:, 0:1], func=ACTF.Identity, scale=nm[:, 0:1], bias=nm[:, 2:3]
            )

        early = [(j, h) for j in range(NJ - TAIL_NODES) for h in range(2)]
        seq = early + [(j, h) for h in range(2) for j in range(NJ - TAIL_NODES, NJ)]
        trb = {}
        ge = {}
        ecs = {}
        acc = {}
        rz = {}
        tet = {}
        et = {}
        mt = {}
        ubt = {}

        def ok(t):
            return 0 <= t < NT

        esort = {}

        def t_sort(t):
            if not ok(t):
                return
            j, h = t // 2, t % 2
            esort[t] = stage.tile([P, 512], F32, name="esort", tag="esort", bufs=2)
            nc.scalar.copy(
                out=esort[t][:].rearrange("p (g u q) -> p g u q", g=2, u=2),
                in_=ech[(h, j // 2)][:].bitcast(F32)[:, j % 2, :].rearrange("p (g q u) -> p g u q", g=2, u=2),
            )

        def t_transpose(t, tag="tr", bufs=1):
            if not ok(t):
                return
            j, h = seq[t]
            ef = ech[(h, j // 2)][:].bitcast(F32)
            if t in esort:
                trb[t] = transposes(esort[t], tag, bufs, True)
            else:
                trb[t] = transposes(ef[:, j % 2, :], tag, bufs)

        def t_regroup(t):
            if not ok(t):
                return
            ge[t] = stage.tile([P, 2, 512], BF16, name="ge", tag="ge", bufs=3, align_bytes=64)
            regroup(ge[t][:].bitcast(F32).rearrange("q g (r u) -> q g r u", u=2), trb[t])

        def t_quantise(t):
            if not ok(t):
                return
            c_ = stage.tile([P, 2, P], U32, name="ec", tag="ec", bufs=4, align_bytes=64)
            s_ = stage.tile([P, 2, P], U8, name="es", tag="es", bufs=4, align_bytes=64)
            nc.vector.quantize_mx(
                out=c_[:].rearrange("q g r -> q (g r)").bitcast(FP8X4),
                scales=s_[:].rearrange("q g r -> q (g r)"),
                in_=ge[t][:].rearrange("q g w -> q (g w)"),
            )
            ecs[t] = (c_, s_)

        def t_agg(t, n2, first=0, last=5):
            if not ok(t):
                return
            j, h = seq[t]
            if first == 0:
                acc[(t, n2)] = psum.tile([P, HALF], F32, name="acc", tag="acc", bufs=4)
            a_ = acc[(t, n2)]
            cols = slice(n2 * HALF, (n2 + 1) * HALF)
            c_, s_ = ecs[t]
            ops = [
                (c_, s_, "WE"),
                (xc[:, h], xs[:, h], "WA"),
                (xrc[:, j], xrs[:, j], "WB"),
            ]
            i = 0
            for lc, ls, w in ops:
                for g in range(2):
                    if first <= i <= last:
                        mx(a_[:], lc[:, g, :], ls[:, g, :], wc[w][:, g, cols], ws[w][:, g, cols], i == 0, i == 5)
                    i += 1

        def t_bn(t, n2):
            if ok(t):
                stats_bn(t, n2, acc[(t, n2)][:])

        def t_aggr(t):
            if ok(t):
                stats_aggr(t)

        def t_e2(t):
            if ok(t):
                stats_e2(t)

        def t_sum(t):
            if ok(t):
                stats_sum(t)

        def t_out(t):
            if ok(t):
                stats_out(t)

        def t_negvar(t):
            if ok(t):
                stats_negvar(t)

        vareps = {}

        def t_vareps(t):
            if not ok(t):
                return
            vareps[t] = small.tile([P, 1], F32, name="vareps", tag="vareps", bufs=3)
            nc.vector.tensor_scalar(
                out=vareps[t][:], in0=negvar[t][:], scalar1=-1.0, scalar2=EPS, op0=ALU.mult, op1=ALU.add
            )

        def t_rstd(t):
            if not ok(t):
                return
            rstd[t] = small.tile([P, 1], F32, name="rstd", tag="rstd", bufs=4)
            nc.gpsimd.tensor_tensor(out=rstd[t][:], in0=vareps[t][:], in1=mhalf[:], op=ALU.pow)

        def t_relu(t, n2):
            if not ok(t):
                return
            if n2 == 0:
                rz[t] = work.tile([P, C], F32, name="rz", tag="rz", bufs=5)
            cols = slice(n2 * HALF, (n2 + 1) * HALF)
            nc.scalar.activation(
                out=rz[t][:, cols], in_=acc[(t, n2)][:], func=ACTF.Relu, bias=nmt[t][:, 0:1], scale=1.0
            )

        whole = slice(0, C)
        halves = [slice(n2 * HALF, (n2 + 1) * HALF) for n2 in range(2)]

        def t_edge_out(t, cols=whole):
            if not ok(t):
                return
            j, h = seq[t]
            nc.vector.scalar_tensor_tensor(
                out=rz[t][:, cols],
                in0=rz[t][:, cols],
                scalar=rstd[t][:, 0:1],
                in1=ech[(h, j // 2)][:, j % 2, cols],
                op0=ALU.mult,
                op1=ALU.add,
            )
            nc.sync.dma_start(out=o1[h][:, j, cols], in_=rz[t][:, cols])

        def t_tanh(t, cols=whole):
            if not ok(t):
                return
            if cols.start == 0:
                tet[t] = work.tile([P, C], F32, name="te", tag="te", bufs=3)
            nc.scalar.activation(out=tet[t][:, cols], in_=rz[t][:, cols], func=ACTF.Tanh, scale=0.5)

        def t_exp(t, cols=whole):
            if not ok(t):
                return
            j, h = seq[t]
            et[t] = den[h] if j == 0 else tet[t]
            nc.scalar.activation(out=et[t][:, cols], in_=tet[t][:, cols], func=ACTF.Exp, scale=0.5)

        def t_u(t):
            if not ok(t) or (t > 0 and seq[t - 1][0] == seq[t][0]):
                return
            j = seq[t][0]
            for n2 in range(2):
                u_ = psum.tile([P, HALF], F32, name="ub", tag="ub", bufs=2)
                cols = slice(n2 * HALF, (n2 + 1) * HALF)
                for g in range(2):
                    mx(u_[:], xrc[:, j, g, :], xrs[:, j, g, :], wc["WV"][:, g, cols], ws["WV"][:, g, cols], g == 0, g == 1)
                ubt[(j, n2)] = u_

        def t_prod(t, n2):
            if not ok(t):
                return
            j, h = seq[t]
            if n2 == 0:
                mt[t] = num[h] if j == 0 else work.tile([P, C], F32, name="mt", tag="mt", bufs=2)
            cols = slice(n2 * HALF, (n2 + 1) * HALF)
            nc.vector.tensor_tensor(out=mt[t][:, cols], in0=et[t][:, cols], in1=ubt[(j, n2)][:], op=ALU.mult)

        def t_den(t, eng=nc.gpsimd, cols=whole):
            if not ok(t) or seq[t][0] == 0:
                return
            h = seq[t][1]
            eng.tensor_tensor(out=den[h][:, cols], in0=den[h][:, cols], in1=et[t][:, cols], op=ALU.add)

        def t_num(t):
            if not ok(t) or seq[t][0] == 0:
                return
            h = seq[t][1]
            nc.vector.tensor_tensor(out=num[h][:], in0=num[h][:], in1=mt[t][:], op=ALU.add)

        start_tags = [("acc", 4), ("ub", 2)]
        for n2 in range(2):
            for w in ("WE", "WA", "WB"):
                load_w(w, 2 * n2)
                load_w(w, 2 * n2 + 1)
                if n2 == 0 and w == "WE":
                    gxf0 = gx[:].bitcast(F32)
                    xf = xn[:].bitcast(F32)
                    for h in range(2):
                        bank = transposes(xf[:, h, :], "acc", 4)
                        regroup(gxf0[:, h, :, :].rearrange("q g (r u) -> q g r u", u=2), bank)
                    nc.vector.quantize_mx(
                        out=xc[:].rearrange("q h g r -> q (h g r)").bitcast(FP8X4),
                        scales=xs[:].rearrange("q h g r -> q (h g r)"),
                        in_=gx[:].rearrange("q h g w -> q (h g w)"),
                    )
                    t_transpose(0, "acc", 4)
                    t_regroup(0)
                    t_transpose(1, "acc", 4)
                    t_regroup(1)
                    for jj in range(4):
                        for g in range(2):
                            xrep_copy(0, jj, g, False)
                    t_quantise(0)
                    t_quantise(1)
                    xrep_quant(0)
                prep_w(w, 2 * n2, start_tags)
                prep_w(w, 2 * n2 + 1, start_tags)
                quant_w(w, n2)
        load_e(0, 1, 2)
        load_w("WV", 0)
        load_w("WV", 1)
        load_e(1)
        load_w("WV", 2)
        load_w("WV", 3)
        load_e(2)

        for jj in range(4):
            for g in range(2):
                xrep_copy(1, jj, g, True)

        uix = {}

        def wu_unit(k):
            u = (k - WU_FIRST_ROUND) // 2
            if (k - WU_FIRST_ROUND) % 2 != 0 or not 0 <= u < 8:
                return None
            return (u // 2, u % 2)

        for k in range(NT):
            if k > 0:
                t_regroup(k + 3)
            t_tanh(k - 3)
            wv = WV_UNITS[k] if k < len(WV_UNITS) else ()
            for u in wv:
                unit_p("WV", u // 2, u % 2)
            t_agg(k, 0)
            t_bn(k, 0)
            if k == 4:
                t_u(0)
            t_agg(k, 1, 0, SPLIT - 1)
            t_sum(k - 1)
            t_agg(k, 1, SPLIT, 5)
            t_out(k - 1)
            t_rstd(k - 2)
            t_den(k - 4, nc.gpsimd, slice(0, DEN_POOL))
            t_prod(k - 4, 0)
            t_relu(k - 1, 0)
            t_negvar(k - 1)
            t_prod(k - 4, 1)
            t_relu(k - 1, 1)
            t_exp(k - 3)
            t_bn(k, 1)
            if k > 0:
                t_quantise(k + 2)
            t_aggr(k)
            if k == 0:
                t_transpose(2, "ub", 2)
                t_transpose(3)
                t_regroup(2)
                t_regroup(3)
                t_quantise(2)
            for i, u in enumerate(wv):
                if u % 4 == 0:
                    new_gw("WV", u // 4)
                if i == 2:
                    t_transpose(k + 4)
                unit_t("WV", u // 2, u % 2, "ub", 2)
                unit_r("WV", u // 2, u % 2, i == 0 or k == 3)
                if u % 4 == 3:
                    quant_w("WV", u // 4)
            if len(wv) < 3:
                t_transpose(k + 4)
            if k != 3:
                t_u(k - 3)
            un = wu_unit(k)
            if un is not None:
                if un[0] % 2 == 0 and un[1] == 0:
                    new_gw("WU", un[0] // 2)
                unit_t("WU", un[0], un[1], "st", 1)
            t_num(k - 4)
            t_den(k - 4, nc.vector, slice(DEN_POOL, C))
            t_e2(k)
            t_vareps(k - 1)
            t_edge_out(k - 2)
            if k == 0:
                xrep_quant(1)
            for a, jj in XREP[k] if k < 3 else ():
                for g in range(2):
                    xrep_copy(a, jj, g, True)
            if k in (2, 3):
                xrep_quant(k)
            if un is not None:
                unit_r("WU", un[0], un[1])
            if k > 1 and un is None:
                t_sort(k + 5)
            if k in (WU_FIRST_ROUND + 8, WU_FIRST_ROUND + 16):
                quant_w("WU", (k - WU_FIRST_ROUND) // 8 - 1)
            if k == 4:
                for a in range(4):
                    load_w("WU", a)
            if k % 4 == 1 and 3 <= (k + 7) // 4 < NJ // 2:
                load_e((k + 7) // 4)

        def x_wu(h, tags):
            for n2 in range(2):
                tag, bufs = tags[n2]
                u_ = psum.tile([P, HALF], F32, name="uix", tag=tag, bufs=bufs)
                cols = halves[n2]
                for g in range(2):
                    mx(u_[:], xc[:, h, g, :], xs[:, h, g, :], wc["WU"][:, g, cols], ws["WU"][:, g, cols], g == 0, g == 1)
                uix[(h, n2)] = u_

        def recip(h):
            for n2 in range(2):
                nc.scalar.activation(
                    out=den[h][:, halves[n2]], in_=dn[(h, n2)][:], func=ACTF.Abs_reciprocal_sqrt, scale=16.0
                )
            for n2 in range(2):
                cols = halves[n2]
                nc.scalar.activation(out=den[h][:, cols], in_=den[h][:, cols], func=ACTF.Square)

        dn = {}

        def den_add(h, src, start, stop):
            for n2 in range(2):
                if start:
                    dn[(h, n2)] = psum.tile([P, HALF], F32, name="dn", tag="acc", bufs=4)
                nc.tensor.matmul(out=dn[(h, n2)][:], lhsT=ident[:], rhs=src[:, halves[n2]], start=start, stop=stop)

        xnew = {}

        def tail_mul(h, n2, eng=nc.vector):
            cols = halves[n2]
            eng.tensor_tensor(out=num[h][:, cols], in0=num[h][:, cols], in1=den[h][:, cols], op=ALU.mult)

        def tail_add(h, n2):
            cols = halves[n2]
            if n2 == 0:
                xnew[h] = work.tile([P, C], F32, name="xnew", tag="rz", bufs=5)
            nc.vector.tensor_tensor(out=xnew[h][:, cols], in0=num[h][:, cols], in1=uix[(h, n2)][:], op=ALU.add)

        def tail_bn(h, n2):
            stats_bn(("x", h), n2, xnew[h][:, halves[n2]])

        def tail_x(h):
            for f in (tail_mul, tail_add, tail_bn):
                f(h, 0)
                f(h, 1)

        def tail_e2(h):
            mv = mvt[("x", h)]
            nc.vector.tensor_scalar(
                out=mv[:, 2:3], in0=mv[:, 0:1], scalar1=mv[:, 0:1], scalar2=mv[:, 1:2], op0=ALU.mult, op1=ALU.add
            )
            stats_sum(("x", h))
            stats_out(("x", h))

        def tail_negvar(h):
            key = ("x", h)
            st = pst[key]
            negvar[key] = small.tile([P, 1], F32, name="negvarx", tag="negvarx", bufs=2)
            nc.vector.tensor_scalar(
                out=negvar[key][:], in0=st[:, 0:1], scalar1=st[:, 0:1], scalar2=st[:, 2:3], op0=ALU.mult, op1=ALU.add
            )

        def tail_rstd(h):
            key = ("x", h)
            varepsx = small.tile([P, 1], F32, name="varepsx", tag="varepsx", bufs=2)
            nc.vector.tensor_scalar(
                out=varepsx[:], in0=negvar[key][:], scalar1=-1.0, scalar2=EPS, op0=ALU.mult, op1=ALU.add
            )
            rstd[key] = small.tile([P, 1], F32, name="rstd", tag="rstd", bufs=4)
            nc.gpsimd.tensor_tensor(out=rstd[key][:], in0=varepsx[:], in1=mhalf[:], op=ALU.pow)
            nbt[key] = small.tile([P, 1], F32, name="nb", tag="nb", bufs=2)
            nc.gpsimd.tensor_tensor(out=nbt[key][:], in0=nmt[key][:, 0:1], in1=rstd[key][:], op=ALU.mult)

        def tail_out(h, n2):
            key = ("x", h)
            cols = halves[n2]
            nc.vector.scalar_tensor_tensor(
                out=xnew[h][:, cols],
                in0=xnew[h][:, cols],
                scalar=rstd[key][:, 0:1],
                in1=xn[:, h, cols],
                op0=ALU.mult,
                op1=ALU.add,
            )
            nc.scalar.activation(
                out=xnew[h][:, cols], in_=xnew[h][:, cols], func=ACTF.Relu, bias=nbt[key][:, 0:1], scale=1.0
            )
            nc.sync.dma_start(out=o0[h][:, cols], in_=xnew[h][:, cols])

        t = NT - 1
        t_tanh(t - 2)
        t_sum(t)
        t_prod(t - 3, 0)
        t_prod(t - 3, 1)
        t_rstd(t - 1)
        den_add(0, den[0], True, False)
        den_add(0, et[t - 3], False, False)
        t_out(t)
        t_relu(t, 0)
        t_negvar(t)
        t_relu(t, 1)
        t_exp(t - 2)
        t_num(t - 3)
        t_vareps(t)
        t_rstd(t)
        t_edge_out(t - 1)
        t_prod(t - 2, 0)
        t_prod(t - 2, 1)
        den_add(1, den[1], True, False)
        t_u(t - 1)
        t_tanh(t - 1)
        t_exp(t - 1)
        for cols in halves:
            t_edge_out(t, cols)
        t_num(t - 2)
        den_add(0, et[t - 1], False, True)
        den_add(1, et[t - 2], False, False)
        t_prod(t - 1, 0)
        t_prod(t - 1, 1)
        for cols in halves:
            t_tanh(t, cols)
        for cols in halves:
            t_exp(t, cols)
        den_add(1, et[t], False, True)
        recip(0)
        t_num(t - 1)
        recip(1)
        t_prod(t, 0)
        t_prod(t, 1)
        x_wu(0, [("tr", 1), ("ub", 2)])
        t_num(t)
        x_wu(1, [("acc", 4), ("acc", 4)])
        tail_x(0)
        tail_mul(1, 0, nc.gpsimd)
        tail_mul(1, 1, nc.gpsimd)
        stats_aggr(("x", 0))
        tail_add(1, 0)
        tail_e2(0)
        tail_add(1, 1)
        tail_bn(1, 0)
        tail_negvar(0)
        tail_bn(1, 1)
        tail_rstd(0)
        stats_aggr(("x", 1))
        tail_e2(1)
        tail_out(0, 0)
        tail_negvar(1)
        tail_rstd(1)
        tail_out(0, 1)
        tail_out(1, 0)
        tail_out(1, 1)
